import numpy as np
import ml_dtypes


def mxq(x, axis, fmt="e4m3"):
    dtype, down = {"e4m3": (ml_dtypes.float8_e4m3fn, 7), "e5m2": (ml_dtypes.float8_e5m2, 14)}[fmt]
    v = np.moveaxis(np.asarray(x, np.float32).astype(ml_dtypes.bfloat16).astype(np.float64), axis, -1)
    blocks = v.reshape(v.shape[:-1] + (-1, 32))
    amax = np.abs(blocks).max(-1, keepdims=True)
    byte = np.maximum(np.where(amax > 0, np.frexp(amax)[1] - 1 + 127, 0) - down, 1)
    scale = np.exp2(byte - 127.0)
    codes = (blocks / scale).astype(np.float32).astype(dtype).astype(np.float64)
    return np.moveaxis((codes * scale).reshape(v.shape), -1, axis)


WIDE = False


def mx_kscale(k):
    if not WIDE:
        return np.ones(k)
    levels = np.array([10, -10, 5, -5, 0])
    a = np.random.permutation(np.resize(levels, k // 512 * 4)).reshape(k // 512, 4)
    idx = np.arange(k)
    return np.exp2(a[idx // 512, idx % 128 // 32])


BF16 = ml_dtypes.bfloat16


def bf(x):
    return np.asarray(x, np.float32).astype(BF16)


def f64(x):
    return np.asarray(x).astype(np.float64)


B, T, I, H, U, V = 4, 256, 256, 512, 1024, 1024
LECUN_A = 1.7159
LECUN_B = 0.666


def lecun_tanh(v):
    return LECUN_A * np.tanh(LECUN_B * v)


def sigmoid(v):
    return 1.0 / (1.0 + np.exp(-v))


def setup_inputs():
    s = mx_kscale(U)
    return {
        "h1": bf(lecun_tanh(np.random.standard_normal((B, T, U))) * s),
        "ts": bf(np.random.uniform(size=(B, T))),
        "W1": bf(np.random.standard_normal((U, V)) / np.sqrt(U) / s[:, None]),
        "b1": bf(np.random.standard_normal(V) * 0.3),
        "W_ff1": bf(np.random.standard_normal((V, H)) / np.sqrt(V)),
        "b_ff1": bf(np.random.standard_normal(H) * 0.3),
        "W_ff2": bf(np.random.standard_normal((V, H)) / np.sqrt(V)),
        "b_ff2": bf(np.random.standard_normal(H) * 0.3),
        "W_ta": bf(np.random.standard_normal((V, H)) / np.sqrt(V)),
        "b_ta": bf(np.random.standard_normal(H) * 0.3),
        "W_tb": bf(np.random.standard_normal((V, H)) / np.sqrt(V)),
        "b_tb": bf(np.random.standard_normal(H) * 0.3),
    }


def reference(h1, ts, W1, b1, W_ff1, b_ff1, W_ff2, b_ff2, W_ta, b_ta, W_tb, b_tb):
    x = lecun_tanh((mxq(f64(h1), 2, "e4m3") @ mxq(f64(W1), 0, "e4m3")) + f64(b1))
    xq = mxq(x, 2, "e4m3")
    ff1 = np.tanh((xq @ mxq(f64(W_ff1), 0, "e4m3")) + f64(b_ff1))
    ff2 = np.tanh((xq @ mxq(f64(W_ff2), 0, "e4m3")) + f64(b_ff2))
    t_a = (xq @ mxq(f64(W_ta), 0, "e4m3")) + f64(b_ta)
    t_b = (xq @ mxq(f64(W_tb), 0, "e4m3")) + f64(b_tb)
    t_interp = sigmoid(t_a * f64(ts)[:, :, None] + t_b)
    return ff1 * (1.0 - t_interp) + t_interp * ff2

@@ -1,0 +1,246 @@
+from contextlib import ExitStack
+
+import concourse.mybir as mybir
+from concourse.masks import make_identity
+
+F32 = mybir.dt.float32
+BF16 = mybir.dt.bfloat16
+U32 = mybir.dt.uint32
+U8 = mybir.dt.uint8
+FP8X4 = mybir.dt.float8_e4m3fn_x4
+ACT = mybir.ActivationFunctionType
+ALU = mybir.AluOpType
+
+P = 128
+TOK = 1024
+U_DIM = 1024
+V_DIM = 1024
+H_DIM = 512
+FLOPS = 2 * TOK * U_DIM * V_DIM + 4 * 2 * TOK * V_DIM * H_DIM
+
+W1_ON_SCALAR = ((0, 1),)
+HEAD_ON_SCALAR = ((1, 1), (2, 1), (3, 0), (3, 1))
+
+
+def tile_cfccell_pa_kernel(
+    tc, h1, ts, W1, b1, W_ff1, b_ff1, W_ff2, b_ff2, W_ta, b_ta, W_tb, b_tb, out
+):
+    nc = tc.nc
+    h1f = h1.flatten_outer_dims()
+    outf = out.flatten_outer_dims()
+    ts_row = ts.rearrange("b t -> (b t)")
+    head_w = [W_ff1, W_ff2, W_ta, W_tb]
+    head_b = [b_ff1, b_ff2, b_ta, b_tb]
+
+    with ExitStack() as ctx:
+        keep = ctx.enter_context(tc.tile_pool(name="keep", bufs=1))
+        raw = ctx.enter_context(tc.tile_pool(name="raw", bufs=5))
+        grp = ctx.enter_context(tc.tile_pool(name="grp", bufs=4))
+        thp = ctx.enter_context(tc.tile_pool(name="thp", bufs=2))
+        work = ctx.enter_context(tc.tile_pool(name="work", bufs=3))
+        psum = ctx.enter_context(tc.psum_pool(name="psum", bufs=8))
+
+        bias_rows = keep.tile([P, P], BF16, name="bias_rows")
+        nc.vector.memset(bias_rows[:], 0.0)
+        nc.scalar.dma_start(out=bias_rows[0:8, :], in_=b1.rearrange("(r c) -> r c", c=P))
+        for h in range(4):
+            nc.scalar.dma_start(
+                out=bias_rows[8 + 4 * h : 12 + 4 * h, :],
+                in_=head_b[h].rearrange("(r c) -> r c", c=P),
+            )
+        ident_f = keep.tile([P, P], F32, name="ident_f")
+        make_identity(nc, ident_f[:])
+        ident_b = keep.tile([P, P], BF16, name="ident_b")
+        make_identity(nc, ident_b[:])
+
+        w1_raw = []
+        for g in range(2):
+            t_raw = raw.tile([P, 4, 1024], BF16, name="w1_raw%d" % g, tag="raw")
+            for u in range(2):
+                r0 = 512 * g + 256 * u
+                nc.sync.dma_start(
+                    out=t_raw[:, 2 * u : 2 * u + 2, :],
+                    in_=W1[r0 : r0 + 256, :].rearrange("(q e) c -> q e c", e=2),
+                )
+            w1_raw.append(t_raw)
+        h1_raw = []
+        for n in range(2):
+            t_raw = raw.tile([P, 4, 1024], BF16, name="h1_raw%d" % n, tag="raw")
+            nc.sync.dma_start(
+                out=t_raw[:],
+                in_=h1f[512 * n : 512 * n + 512, :].rearrange("(t p) u -> p t u", p=P),
+            )
+            h1_raw.append(t_raw)
+        ts_b = keep.tile([P, TOK], BF16, name="ts_b")
+        nc.sync.dma_start(out=ts_b[:], in_=ts_row.partition_broadcast(P))
+        hd_raw = []
+        for h in range(4):
+            t_raw = raw.tile([P, 2, 4, 512], BF16, name="hd_raw%d" % h, tag="raw")
+            for g in range(2):
+                nc.sync.dma_start(
+                    out=t_raw[:, g, :, :],
+                    in_=head_w[h][512 * g : 512 * g + 512, :].rearrange("(t p) n -> p t n", p=P),
+                )
+            hd_raw.append(t_raw)
+
+        pb = psum.tile([P, P], BF16, name="pb", tag="bank")
+        nc.tensor.transpose(pb[:], bias_rows[:], ident_b[:])
+        bias_t = keep.tile([P, 24], F32, name="bias_t")
+        nc.vector.tensor_copy(out=bias_t[:], in_=pb[:, 0:24])
+        b1s = keep.tile([P, 8], F32, name="b1s")
+        nc.vector.tensor_scalar_mul(out=b1s[:], in0=bias_t[:, 0:8], scalar1=0.666)
+
+        def regroup(on_scalar, src, name):
+            g_t = grp.tile([P, 2048], BF16, name=name, tag="grp", align_bytes=64)
+            dst = g_t[:].rearrange("p (c i t) -> p c t i", i=4, t=4)
+            s_v = src.rearrange("p t (c i) -> p c t i", i=4)
+            if on_scalar:
+                nc.scalar.copy(out=dst, in_=s_v)
+            else:
+                nc.vector.tensor_copy(out=dst, in_=s_v)
+            return g_t
+
+        def quantise(g_t, name):
+            codes = keep.tile([P, 512], U32, name=name + "_c", align_bytes=64)
+            scales = keep.tile([P, 512], U8, name=name + "_s", align_bytes=64)
+            nc.vector.quantize_mx(out=codes[:].bitcast(FP8X4), scales=scales[:], in_=g_t[:])
+            return (codes, scales)
+
+        def mx_group(stat, cols, mov):
+            acc = psum.tile([P, 512], F32, name="acc", tag="bank")
+            for g in range(2):
+                nc.tensor.matmul_mx(
+                    out=acc[:],
+                    lhsT=stat[g][0][:, cols].bitcast(FP8X4),
+                    lhsT_scale=stat[g][1][:, cols],
+                    rhs=mov[g][0][:].bitcast(FP8X4),
+                    rhs_scale=mov[g][1][:],
+                    start=(g == 0),
+                    stop=(g == 1),
+                )
+            return acc
+
+        w1_q = {}
+        w1_g = {}
+        for g in range(2):
+            for cc in range(2):
+                w1_g[(g, cc)] = regroup(
+                    (g, cc) in W1_ON_SCALAR,
+                    w1_raw[g][:, :, 512 * cc : 512 * cc + 512],
+                    "w1g%d%d" % (g, cc),
+                )
+        for g in range(2):
+            for cc in range(2):
+                w1_q[(g, cc)] = quantise(w1_g[(g, cc)], "w1q%d%d" % (g, cc))
+
+        h1_q = {}
+        for n in range(2):
+            for g in range(2):
+                hg = grp.tile([P, 2048], BF16, name="h1g%d%d" % (g, n), tag="grp", align_bytes=64)
+                hgw = hg[:].bitcast(F32).rearrange("p (r u) -> p r u", u=2)
+                for hh in range(2):
+                    bank = psum.tile([P, 2, 256], F32, name="h1t", tag="bank")
+                    for u in range(2):
+                        for j in range(2):
+                            c0 = 256 * g + 128 * u
+                            nc.tensor.transpose(
+                                bank[:, u, 128 * j : 128 * j + 128],
+                                h1_raw[n][:, 2 * hh + j, :].bitcast(F32)[:, c0 : c0 + 128],
+                                ident_f[:],
+                            )
+                    nc.scalar.copy(
+                        out=hgw[:, 256 * hh : 256 * hh + 256, :],
+                        in_=bank[:].rearrange("p u r -> p r u"),
+                    )
+                h1_q[(g, n)] = quantise(hg, "h1q%d%d" % (g, n))
+
+        x_q = {}
+        for n in range(2):
+            for gv in range(2):
+                th = thp.tile([P, 4, 512], F32, name="th", tag="th")
+                for t in range(4):
+                    m = 4 * gv + t
+                    acc = mx_group(
+                        [w1_q[(0, gv)], w1_q[(1, gv)]],
+                        slice(128 * t, 128 * t + 128),
+                        [h1_q[(0, n)], h1_q[(1, n)]],
+                    )
+                    nc.scalar.activation(
+                        out=th[:, t, :], in_=acc[:], func=ACT.Tanh, bias=b1s[:, m : m + 1], scale=0.666
+                    )
+                xg = grp.tile([P, 2048], BF16, name="xg%d%d" % (gv, n), tag="grp", align_bytes=64)
+                nc.vector.tensor_scalar_mul(
+                    out=xg[:].rearrange("p (r t) -> p r t", t=4),
+                    in0=th[:].rearrange("p t r -> p r t"),
+                    scalar1=1.7159,
+                )
+                x_q[(gv, n)] = quantise(xg, "xq%d%d" % (gv, n))
+
+        units = [(hq, n) for n in range(2) for hq in range(4)]
+
+        def head_weights(h):
+            tiles = [
+                regroup((h, g) in HEAD_ON_SCALAR, hd_raw[h][:, g, :, :], "hg%d%d" % (h, g))
+                for g in range(2)
+            ]
+            return [quantise(tiles[g], "hq%d%d" % (h, g)) for g in range(2)]
+
+        def head_group(wq, hq, n):
+            return mx_group(wq, slice(128 * hq, 128 * hq + 128), [x_q[(0, n)], x_q[(1, n)]])
+
+        def bias_col(h, hq):
+            c = 8 + 4 * h + hq
+            return bias_t[:, c : c + 1]
+
+        ff1 = {}
+        wq = head_weights(0)
+        for hq, n in units:
+            acc = head_group(wq, hq, n)
+            ff1[(hq, n)] = keep.tile([P, 512], F32, name="ff1_%d%d" % (hq, n))
+            nc.scalar.activation(out=ff1[(hq, n)][:], in_=acc[:], func=ACT.Tanh, bias=bias_col(0, hq), scale=1.0)
+
+        dif = {}
+        wq = head_weights(1)
+        for hq, n in units:
+            acc = head_group(wq, hq, n)
+            ff2 = work.tile([P, 512], F32, name="ff2", tag="ff2")
+            nc.scalar.activation(out=ff2[:], in_=acc[:], func=ACT.Tanh, bias=bias_col(1, hq), scale=1.0)
+            dif[(hq, n)] = keep.tile([P, 512], F32, name="dif_%d%d" % (hq, n))
+            nc.vector.tensor_sub(out=dif[(hq, n)][:], in0=ff2[:], in1=ff1[(hq, n)][:])
+
+        v1 = {}
+        wq = head_weights(2)
+        for hq, n in units:
+            acc = head_group(wq, hq, n)
+            v1[(hq, n)] = keep.tile([P, 512], F32, name="v1_%d%d" % (hq, n))
+            nc.vector.scalar_tensor_tensor(
+                out=v1[(hq, n)][:],
+                in0=acc[:],
+                scalar=bias_col(2, hq),
+                in1=ts_b[:, 512 * n : 512 * n + 512],
+                op0=ALU.add,
+                op1=ALU.mult,
+            )
+
+        wq = head_weights(3)
+        for hq, n in units:
+            acc = head_group(wq, hq, n)
+            z = work.tile([P, 512], F32, name="z", tag="z")
+            nc.vector.tensor_add(out=z[:], in0=acc[:], in1=v1[(hq, n)][:])
+            gate = work.tile([P, 512], F32, name="gate", tag="gate")
+            nc.scalar.activation(out=gate[:], in_=z[:], func=ACT.Sigmoid, bias=bias_col(3, hq), scale=1.0)
+            e = work.tile([P, 512], F32, name="e", tag="e")
+            nc.vector.tensor_mul(out=e[:], in0=gate[:], in1=dif[(hq, n)][:])
+            o = work.tile([P, 512], F32, name="o", tag="o")
+            nc.vector.tensor_add(out=o[:], in0=e[:], in1=ff1[(hq, n)][:])
+            ot = psum.tile([P, 4, P], F32, name="ot", tag="bank")
+            for tt in range(4):
+                nc.tensor.transpose(ot[:, tt, :], o[:, 128 * tt : 128 * tt + 128], ident_f[:])
+            ost = work.tile([P, 4, P], F32, name="ost", tag="ost")
+            nc.scalar.copy(out=ost[:], in_=ot[:])
+            nc.sync.dma_start(
+                out=outf[512 * n : 512 * n + 512, 128 * hq : 128 * hq + 128].rearrange(
+                    "(t p) h -> p t h", p=P
+                ),
+                in_=ost[:],
+            )

@@ -18,8 +18,9 @@ V_DIM = 1024
 H_DIM = 512
 FLOPS = 2 * TOK * U_DIM * V_DIM + 4 * 2 * TOK * V_DIM * H_DIM
 
-W1_ON_SCALAR = ((0, 1),)
-HEAD_ON_SCALAR = ((1, 1), (2, 1), (3, 0), (3, 1))
+FF1, FF2, TA, TB = 0, 1, 2, 3
+TRICK = False
+GD = False
 
 
 def tile_cfccell_pa_kernel(
@@ -39,6 +40,7 @@ def tile_cfccell_pa_kernel(
         thp = ctx.enter_context(tc.tile_pool(name="thp", bufs=2))
         work = ctx.enter_context(tc.tile_pool(name="work", bufs=3))
         psum = ctx.enter_context(tc.psum_pool(name="psum", bufs=8))
+        ctx.enter_context(tc.manual_schedule())
 
         bias_rows = keep.tile([P, P], BF16, name="bias_rows")
         nc.vector.memset(bias_rows[:], 0.0)
@@ -48,10 +50,10 @@ def tile_cfccell_pa_kernel(
                 out=bias_rows[8 + 4 * h : 12 + 4 * h, :],
                 in_=head_b[h].rearrange("(r c) -> r c", c=P),
             )
-        ident_f = keep.tile([P, P], F32, name="ident_f")
-        make_identity(nc, ident_f[:])
         ident_b = keep.tile([P, P], BF16, name="ident_b")
         make_identity(nc, ident_b[:])
+        ident_f = keep.tile([P, P], F32, name="ident_f")
+        make_identity(nc, ident_f[:])
 
         w1_raw = []
         for g in range(2):
@@ -72,72 +74,67 @@ def tile_cfccell_pa_kernel(
             )
             h1_raw.append(t_raw)
         ts_b = keep.tile([P, TOK], BF16, name="ts_b")
-        nc.sync.dma_start(out=ts_b[:], in_=ts_row.partition_broadcast(P))
-        hd_raw = []
-        for h in range(4):
+        hd_raw = {}
+
+        def load_head(h):
             t_raw = raw.tile([P, 2, 4, 512], BF16, name="hd_raw%d" % h, tag="raw")
             for g in range(2):
                 nc.sync.dma_start(
                     out=t_raw[:, g, :, :],
                     in_=head_w[h][512 * g : 512 * g + 512, :].rearrange("(t p) n -> p t n", p=P),
                 )
-            hd_raw.append(t_raw)
+            hd_raw[h] = t_raw
 
-        pb = psum.tile([P, P], BF16, name="pb", tag="bank")
-        nc.tensor.transpose(pb[:], bias_rows[:], ident_b[:])
-        bias_t = keep.tile([P, 24], F32, name="bias_t")
-        nc.vector.tensor_copy(out=bias_t[:], in_=pb[:, 0:24])
-        b1s = keep.tile([P, 8], F32, name="b1s")
-        nc.vector.tensor_scalar_mul(out=b1s[:], in0=bias_t[:, 0:8], scalar1=0.666)
+        load_head(FF1)
+        load_head(TA)
+        nc.sync.dma_start(out=ts_b[:], in_=ts_row.partition_broadcast(P))
+        load_head(TB)
+        load_head(FF2)
 
-        def regroup(on_scalar, src, name):
-            g_t = grp.tile([P, 2048], BF16, name=name, tag="grp", align_bytes=64)
+        grouped = {}
+        quant = {}
+
+        def regroup(eng, key, src):
+            g_t = grp.tile([P, 2048], BF16, name="g_%s_%d%d" % key, tag="grp", align_bytes=64)
             dst = g_t[:].rearrange("p (c i t) -> p c t i", i=4, t=4)
             s_v = src.rearrange("p t (c i) -> p c t i", i=4)
-            if on_scalar:
+            if eng == "S":
                 nc.scalar.copy(out=dst, in_=s_v)
             else:
                 nc.vector.tensor_copy(out=dst, in_=s_v)
-            return g_t
+            grouped[key] = g_t
 
-        def quantise(g_t, name):
-            codes = keep.tile([P, 512], U32, name=name + "_c", align_bytes=64)
-            scales = keep.tile([P, 512], U8, name=name + "_s", align_bytes=64)
-            nc.vector.quantize_mx(out=codes[:].bitcast(FP8X4), scales=scales[:], in_=g_t[:])
-            return (codes, scales)
+        def r_w1(eng, g, cc):
+            regroup(eng, ("w", g, cc), w1_raw[g][:, :, 512 * cc : 512 * cc + 512])
+
+        def r_hd(eng, h, g):
+            regroup(eng, ("h", h, g), hd_raw[h][:, g, :, :])
+
+        def q(key):
+            codes = keep.tile([P, 512], U32, name="c_%s_%d%d" % key, align_bytes=64)
+            scales = keep.tile([P, 512], U8, name="s_%s_%d%d" % key, align_bytes=64)
+            nc.vector.quantize_mx(
+                out=codes[:].bitcast(FP8X4), scales=scales[:], in_=grouped[key][:]
+            )
+            quant[key] = (codes, scales)
 
         def mx_group(stat, cols, mov):
             acc = psum.tile([P, 512], F32, name="acc", tag="bank")
             for g in range(2):
                 nc.tensor.matmul_mx(
                     out=acc[:],
-                    lhsT=stat[g][0][:, cols].bitcast(FP8X4),
-                    lhsT_scale=stat[g][1][:, cols],
-                    rhs=mov[g][0][:].bitcast(FP8X4),
-                    rhs_scale=mov[g][1][:],
+                    lhsT=quant[stat[g]][0][:, cols].bitcast(FP8X4),
+                    lhsT_scale=quant[stat[g]][1][:, cols],
+                    rhs=quant[mov[g]][0][:].bitcast(FP8X4),
+                    rhs_scale=quant[mov[g]][1][:],
                     start=(g == 0),
                     stop=(g == 1),
                 )
             return acc
 
-        w1_q = {}
-        w1_g = {}
-        for g in range(2):
-            for cc in range(2):
-                w1_g[(g, cc)] = regroup(
-                    (g, cc) in W1_ON_SCALAR,
-                    w1_raw[g][:, :, 512 * cc : 512 * cc + 512],
-                    "w1g%d%d" % (g, cc),
-                )
-        for g in range(2):
-            for cc in range(2):
-                w1_q[(g, cc)] = quantise(w1_g[(g, cc)], "w1q%d%d" % (g, cc))
-
-        h1_q = {}
-        for n in range(2):
+        def h1_transposes(n):
+            banks = {}
             for g in range(2):
-                hg = grp.tile([P, 2048], BF16, name="h1g%d%d" % (g, n), tag="grp", align_bytes=64)
-                hgw = hg[:].bitcast(F32).rearrange("p (r u) -> p r u", u=2)
                 for hh in range(2):
                     bank = psum.tile([P, 2, 256], F32, name="h1t", tag="bank")
                     for u in range(2):
@@ -148,99 +145,207 @@ def tile_cfccell_pa_kernel(
                                 h1_raw[n][:, 2 * hh + j, :].bitcast(F32)[:, c0 : c0 + 128],
                                 ident_f[:],
                             )
-                    nc.scalar.copy(
-                        out=hgw[:, 256 * hh : 256 * hh + 256, :],
-                        in_=bank[:].rearrange("p u r -> p r u"),
-                    )
-                h1_q[(g, n)] = quantise(hg, "h1q%d%d" % (g, n))
+                    banks[(g, hh)] = bank
+            return banks
 
-        x_q = {}
-        for n in range(2):
-            for gv in range(2):
-                th = thp.tile([P, 4, 512], F32, name="th", tag="th")
-                for t in range(4):
-                    m = 4 * gv + t
-                    acc = mx_group(
-                        [w1_q[(0, gv)], w1_q[(1, gv)]],
-                        slice(128 * t, 128 * t + 128),
-                        [h1_q[(0, n)], h1_q[(1, n)]],
-                    )
-                    nc.scalar.activation(
-                        out=th[:, t, :], in_=acc[:], func=ACT.Tanh, bias=b1s[:, m : m + 1], scale=0.666
-                    )
-                xg = grp.tile([P, 2048], BF16, name="xg%d%d" % (gv, n), tag="grp", align_bytes=64)
-                nc.vector.tensor_scalar_mul(
-                    out=xg[:].rearrange("p (r t) -> p r t", t=4),
-                    in0=th[:].rearrange("p t r -> p r t"),
-                    scalar1=1.7159,
+        def h1_out(eng, n, g, banks):
+            hg = grp.tile([P, 2048], BF16, name="g_a_%d%d" % (g, n), tag="grp", align_bytes=64)
+            hgw = hg[:].bitcast(F32).rearrange("p (r u) -> p r u", u=2)
+            for hh in range(2):
+                dst = hgw[:, 256 * hh : 256 * hh + 256, :]
+                s_v = banks[(g, hh)][:].rearrange("p u r -> p r u")
+                if eng == "S":
+                    nc.scalar.copy(out=dst, in_=s_v)
+                else:
+                    nc.vector.tensor_copy(out=dst, in_=s_v)
+            grouped[("a", g, n)] = hg
+
+        tanh_x = {}
+
+        def stage1(n, gv):
+            th = thp.tile([P, 4, 512], F32, name="th", tag="th")
+            for t in range(4):
+                m = 4 * gv + t
+                acc = mx_group(
+                    [("w", 0, gv), ("w", 1, gv)],
+                    slice(128 * t, 128 * t + 128),
+                    [("a", 0, n), ("a", 1, n)],
                 )
-                x_q[(gv, n)] = quantise(xg, "xq%d%d" % (gv, n))
+                nc.scalar.activation(
+                    out=th[:, t, :], in_=acc[:], func=ACT.Tanh, bias=b1s[:, m : m + 1], scale=0.666
+                )
+            tanh_x[(gv, n)] = th
 
-        units = [(hq, n) for n in range(2) for hq in range(4)]
+        def x_regroup(gv, n):
+            xg = grp.tile([P, 2048], BF16, name="g_x_%d%d" % (gv, n), tag="grp", align_bytes=64)
+            nc.vector.tensor_scalar_mul(
+                out=xg[:].rearrange("p (r t) -> p r t", t=4),
+                in0=tanh_x[(gv, n)][:].rearrange("p t r -> p r t"),
+                scalar1=1.7159,
+            )
+            grouped[("x", gv, n)] = xg
 
-        def head_weights(h):
-            tiles = [
-                regroup((h, g) in HEAD_ON_SCALAR, hd_raw[h][:, g, :, :], "hg%d%d" % (h, g))
-                for g in range(2)
-            ]
-            return [quantise(tiles[g], "hq%d%d" % (h, g)) for g in range(2)]
-
-        def head_group(wq, hq, n):
-            return mx_group(wq, slice(128 * hq, 128 * hq + 128), [x_q[(0, n)], x_q[(1, n)]])
+        def head_group(h, unit):
+            hq, n = unit
+            return mx_group(
+                [("h", h, 0), ("h", h, 1)],
+                slice(128 * hq, 128 * hq + 128),
+                [("x", 0, n), ("x", 1, n)],
+            )
 
         def bias_col(h, hq):
             c = 8 + 4 * h + hq
             return bias_t[:, c : c + 1]
 
+        r_w1("V", 0, 0)
+        r_w1("S", 0, 1)
+        pb = psum.tile([P, P], BF16, name="pb", tag="bank")
+        nc.tensor.transpose(pb[:], bias_rows[:], ident_b[:])
+        bias_t = keep.tile([P, 24], F32, name="bias_t")
+        nc.vector.tensor_copy(out=bias_t[:], in_=pb[:, 0:24])
+        b1s = keep.tile([P, 8], F32, name="b1s")
+        nc.vector.tensor_scalar_mul(out=b1s[:], in0=bias_t[:, 0:8], scalar1=0.666)
+        r_w1("V", 1, 0)
+        r_w1("S", 1, 1)
+        q(("w", 0, 0))
+        q(("w", 1, 0))
+        q(("w", 0, 1))
+        q(("w", 1, 1))
+        t0 = h1_transposes(0)
+        t1 = h1_transposes(1)
+        h1_out("S", 0, 0, t0)
+        h1_out("S", 0, 1, t0)
+        q(("a", 0, 0))
+        q(("a", 1, 0))
+        h1_out("V", 1, 0, t1)
+        h1_out("V", 1, 1, t1)
+
+        stage1(0, 0)
+        stage1(0, 1)
+        q(("a", 0, 1))
+        q(("a", 1, 1))
+        x_regroup(0, 0)
+        stage1(1, 0)
+        r_hd("V", FF1, 0)
+        q(("x", 0, 0))
+        x_regroup(1, 0)
+        stage1(1, 1)
+        r_hd("V", FF1, 1)
+        q(("x", 1, 0))
+        q(("h", FF1, 0))
+        x_regroup(0, 1)
+        q(("h", FF1, 1))
+        q(("x", 0, 1))
+        r_hd("S", TA, 0)
+        r_hd("S", TA, 1)
+        x_regroup(1, 1)
+        r_hd("V", TB, 0)
+        q(("x", 1, 1))
+        q(("h", TA, 0))
+        q(("h", TA, 1))
+
+        units = [(hq, n) for n in range(2) for hq in range(4)]
+        n_u = len(units)
         ff1 = {}
-        wq = head_weights(0)
-        for hq, n in units:
-            acc = head_group(wq, hq, n)
-            ff1[(hq, n)] = keep.tile([P, 512], F32, name="ff1_%d%d" % (hq, n))
-            nc.scalar.activation(out=ff1[(hq, n)][:], in_=acc[:], func=ACT.Tanh, bias=bias_col(0, hq), scale=1.0)
-
-        dif = {}
-        wq = head_weights(1)
-        for hq, n in units:
-            acc = head_group(wq, hq, n)
-            ff2 = work.tile([P, 512], F32, name="ff2", tag="ff2")
-            nc.scalar.activation(out=ff2[:], in_=acc[:], func=ACT.Tanh, bias=bias_col(1, hq), scale=1.0)
-            dif[(hq, n)] = keep.tile([P, 512], F32, name="dif_%d%d" % (hq, n))
-            nc.vector.tensor_sub(out=dif[(hq, n)][:], in0=ff2[:], in1=ff1[(hq, n)][:])
-
         v1 = {}
-        wq = head_weights(2)
-        for hq, n in units:
-            acc = head_group(wq, hq, n)
-            v1[(hq, n)] = keep.tile([P, 512], F32, name="v1_%d%d" % (hq, n))
-            nc.vector.scalar_tensor_tensor(
-                out=v1[(hq, n)][:],
-                in0=acc[:],
-                scalar=bias_col(2, hq),
-                in1=ts_b[:, 512 * n : 512 * n + 512],
-                op0=ALU.add,
-                op1=ALU.mult,
-            )
+        acc_f = {}
+        acc_a = {}
+        late = {
+            0: [("S", TB, 1)],
+            1: [("S", FF2, 0)],
+            2: [("q", TB, 0), ("V", FF2, 1)],
+            3: [("q", TB, 1)],
+            5: [("q", FF2, 1)],
+            6: [("q", FF2, 0)],
+        }
+        for i in range(n_u + 1):
+            if i < n_u:
+                acc_f[i] = head_group(FF1, units[i])
+                acc_a[i] = head_group(TA, units[i])
+            if i >= 1:
+                k = i - 1
+                hq, n = units[k]
+                ff1[k] = keep.tile([P, 512], F32, name="ff1_%d" % k)
+                nc.scalar.activation(
+                    out=ff1[k][:], in_=acc_f[k][:], func=ACT.Tanh, bias=bias_col(FF1, hq), scale=1.0
+                )
+                v1[k] = keep.tile([P, 512], F32, name="v1_%d" % k)
+                nc.vector.scalar_tensor_tensor(
+                    out=v1[k][:],
+                    in0=acc_a[k][:],
+                    scalar=bias_col(TA, hq),
+                    in1=ts_b[:, 512 * n : 512 * n + 512],
+                    op0=ALU.add,
+                    op1=ALU.mult,
+                )
+                for what, h, g in late.get(k, []):
+                    if what == "q":
+                        q(("h", h, g))
+                    else:
+                        r_hd(what, h, g)
 
-        wq = head_weights(3)
-        for hq, n in units:
-            acc = head_group(wq, hq, n)
-            z = work.tile([P, 512], F32, name="z", tag="z")
-            nc.vector.tensor_add(out=z[:], in0=acc[:], in1=v1[(hq, n)][:])
-            gate = work.tile([P, 512], F32, name="gate", tag="gate")
-            nc.scalar.activation(out=gate[:], in_=z[:], func=ACT.Sigmoid, bias=bias_col(3, hq), scale=1.0)
-            e = work.tile([P, 512], F32, name="e", tag="e")
-            nc.vector.tensor_mul(out=e[:], in0=gate[:], in1=dif[(hq, n)][:])
-            o = work.tile([P, 512], F32, name="o", tag="o")
-            nc.vector.tensor_add(out=o[:], in0=e[:], in1=ff1[(hq, n)][:])
-            ot = psum.tile([P, 4, P], F32, name="ot", tag="bank")
-            for tt in range(4):
-                nc.tensor.transpose(ot[:, tt, :], o[:, 128 * tt : 128 * tt + 128], ident_f[:])
-            ost = work.tile([P, 4, P], F32, name="ost", tag="ost")
-            nc.scalar.copy(out=ost[:], in_=ot[:])
-            nc.sync.dma_start(
-                out=outf[512 * n : 512 * n + 512, 128 * hq : 128 * hq + 128].rearrange(
-                    "(t p) h -> p t h", p=P
-                ),
-                in_=ost[:],
-            )
+        acc_b = {}
+        acc_2 = {}
+        gate = {}
+        dif = {}
+        res = {}
+        for i in range(n_u + 3):
+            if i < n_u:
+                acc_b[i] = head_group(TB, units[i])
+                acc_2[i] = head_group(FF2, units[i])
+            if 3 <= i:
+                k = i - 3
+                ot = psum.tile([P, 4, P], F32, name="ot", tag="bank")
+                for tt in range(4):
+                    cols = slice(128 * tt, 128 * tt + 128)
+                    if TRICK:
+                        nc.tensor.matmul(
+                            out=ot[:, tt, :], lhsT=ff1[k][:, cols], rhs=ident_f[:],
+                            is_transpose=True, start=True, stop=False,
+                        )
+                        nc.tensor.matmul(
+                            out=ot[:, tt, :], lhsT=res[k][:, cols], rhs=ident_f[:],
+                            is_transpose=True, start=False, stop=True,
+                        )
+                    else:
+                        nc.tensor.transpose(ot[:, tt, :], res[k][:, cols], ident_f[:])
+            if 1 <= i <= n_u:
+                k = i - 1
+                hq, n = units[k]
+                z = work.tile([P, 512], F32, name="z", tag="z")
+                nc.vector.tensor_add(out=z[:], in0=acc_b[k][:], in1=v1[k][:])
+                ff2 = work.tile([P, 512], F32, name="ff2", tag="ff2")
+                nc.scalar.activation(
+                    out=ff2[:], in_=acc_2[k][:], func=ACT.Tanh, bias=bias_col(FF2, hq), scale=1.0
+                )
+                gate[k] = work.tile([P, 512], F32, name="gate", tag="gate")
+                nc.scalar.activation(
+                    out=gate[k][:], in_=z[:], func=ACT.Sigmoid, bias=bias_col(TB, hq), scale=1.0
+                )
+            if 2 <= i <= n_u + 1:
+                k = i - 2
+                e = work.tile([P, 512], F32, name="e", tag="e")
+                nc.vector.tensor_mul(out=e[:], in0=gate[k][:], in1=dif[k][:])
+                if TRICK:
+                    res[k] = e
+                else:
+                    res[k] = work.tile([P, 512], F32, name="o", tag="o")
+                    nc.vector.tensor_add(out=res[k][:], in0=e[:], in1=ff1[k][:])
+            if 1 <= i <= n_u:
+                k = i - 1
+                dif[k] = work.tile([P, 512], F32, name="dif", tag="dif")
+                if GD:
+                    nc.gpsimd.tensor_tensor(out=dif[k][:], in0=ff2[:], in1=ff1[k][:], op=ALU.subtract)
+                else:
+                    nc.vector.tensor_sub(out=dif[k][:], in0=ff2[:], in1=ff1[k][:])
+            if 3 <= i:
+                k = i - 3
+                hq, n = units[k]
+                ost = work.tile([P, 4, P], F32, name="ost", tag="ost")
+                nc.scalar.copy(out=ost[:], in_=ot[:])
+                nc.sync.dma_start(
+                    out=outf[512 * n : 512 * n + 512, 128 * hq : 128 * hq + 128].rearrange(
+                        "(t p) h -> p t h", p=P
+                    ),
+                    in_=ost[:],
+                )

@@ -19,7 +19,7 @@ H_DIM = 512
 FLOPS = 2 * TOK * U_DIM * V_DIM + 4 * 2 * TOK * V_DIM * H_DIM
 
 FF1, FF2, TA, TB = 0, 1, 2, 3
-TRICK = False
+TRICK = True
 GD = False
 
 
@@ -50,6 +50,10 @@ def tile_cfccell_pa_kernel(
                 out=bias_rows[8 + 4 * h : 12 + 4 * h, :],
                 in_=head_b[h].rearrange("(r c) -> r c", c=P),
             )
+        warm = keep.tile([P, 1], F32, name="warm")
+        nc.vector.memset(warm[:], 0.0)
+        warm_out = keep.tile([P, 1], F32, name="warm_out")
+        nc.scalar.activation(out=warm_out[:], in_=warm[:], func=ACT.Sigmoid)
         ident_b = keep.tile([P, P], BF16, name="ident_b")
         make_identity(nc, ident_b[:])
         ident_f = keep.tile([P, P], F32, name="ident_f")
@@ -87,8 +91,8 @@ def tile_cfccell_pa_kernel(
 
         load_head(FF1)
         load_head(TA)
-        nc.sync.dma_start(out=ts_b[:], in_=ts_row.partition_broadcast(P))
         load_head(TB)
+        nc.sync.dma_start(out=ts_b[:], in_=ts_row.partition_broadcast(P))
         load_head(FF2)
 
         grouped = {}
@@ -217,32 +221,33 @@ def tile_cfccell_pa_kernel(
         h1_out("S", 0, 1, t0)
         q(("a", 0, 0))
         q(("a", 1, 0))
-        h1_out("V", 1, 0, t1)
-        h1_out("V", 1, 1, t1)
+        h1_out("S", 1, 0, t1)
+        h1_out("S", 1, 1, t1)
 
         stage1(0, 0)
         stage1(0, 1)
         q(("a", 0, 1))
         q(("a", 1, 1))
+        r_hd("V", FF1, 0)
         x_regroup(0, 0)
         stage1(1, 0)
-        r_hd("V", FF1, 0)
+        r_hd("V", FF1, 1)
         q(("x", 0, 0))
         x_regroup(1, 0)
         stage1(1, 1)
-        r_hd("V", FF1, 1)
-        q(("x", 1, 0))
         q(("h", FF1, 0))
-        x_regroup(0, 1)
+        r_hd("V", TA, 0)
+        q(("x", 1, 0))
         q(("h", FF1, 1))
+        x_regroup(0, 1)
+        r_hd("V", TA, 1)
         q(("x", 0, 1))
-        r_hd("S", TA, 0)
-        r_hd("S", TA, 1)
-        x_regroup(1, 1)
-        r_hd("V", TB, 0)
-        q(("x", 1, 1))
+        r_hd("S", TB, 0)
+        r_hd("S", TB, 1)
         q(("h", TA, 0))
+        x_regroup(1, 1)
         q(("h", TA, 1))
+        q(("x", 1, 1))
 
         units = [(hq, n) for n in range(2) for hq in range(4)]
         n_u = len(units)
@@ -251,9 +256,8 @@ def tile_cfccell_pa_kernel(
         acc_f = {}
         acc_a = {}
         late = {
-            0: [("S", TB, 1)],
-            1: [("S", FF2, 0)],
-            2: [("q", TB, 0), ("V", FF2, 1)],
+            1: [("S", FF2, 0), ("q", TB, 0)],
+            2: [("V", FF2, 1)],
             3: [("q", TB, 1)],
             5: [("q", FF2, 1)],
             6: [("q", FF2, 0)],

@@ -183,8 +183,8 @@ def tile_cfccell_pa_kernel(
         def x_regroup(gv, n):
             xg = grp.tile([P, 2048], BF16, name="g_x_%d%d" % (gv, n), tag="grp", align_bytes=64)
             nc.vector.tensor_scalar_mul(
-                out=xg[:].rearrange("p (r t) -> p r t", t=4),
-                in0=tanh_x[(gv, n)][:].rearrange("p t r -> p r t"),
+                out=xg[:].rearrange("p (r i t) -> p r t i", i=4, t=4),
+                in0=tanh_x[(gv, n)][:].rearrange("p t (r i) -> p r t i", i=4),
                 scalar1=1.7159,
             )
             grouped[("x", gv, n)] = xg

@@ -36,7 +36,7 @@ def tile_cfccell_pa_kernel(
     with ExitStack() as ctx:
         keep = ctx.enter_context(tc.tile_pool(name="keep", bufs=1))
         raw = ctx.enter_context(tc.tile_pool(name="raw", bufs=5))
-        grp = ctx.enter_context(tc.tile_pool(name="grp", bufs=4))
+        grp = ctx.enter_context(tc.tile_pool(name="grp", bufs=6))
         thp = ctx.enter_context(tc.tile_pool(name="thp", bufs=2))
         work = ctx.enter_context(tc.tile_pool(name="work", bufs=3))
         psum = ctx.enter_context(tc.psum_pool(name="psum", bufs=8))
@@ -239,12 +239,12 @@ def tile_cfccell_pa_kernel(
         r_hd("V", TA, 0)
         q(("x", 1, 0))
         q(("h", FF1, 1))
-        x_regroup(0, 1)
-        r_hd("V", TA, 1)
-        q(("x", 0, 1))
+        r_hd("S", TA, 1)
         r_hd("S", TB, 0)
         r_hd("S", TB, 1)
+        x_regroup(0, 1)
         q(("h", TA, 0))
+        q(("x", 0, 1))
         x_regroup(1, 1)
         q(("h", TA, 1))
         q(("x", 1, 1))
@@ -317,14 +317,21 @@ def tile_cfccell_pa_kernel(
                 k = i - 1
                 hq, n = units[k]
                 z = work.tile([P, 512], F32, name="z", tag="z")
-                nc.vector.tensor_add(out=z[:], in0=acc_b[k][:], in1=v1[k][:])
+                nc.vector.scalar_tensor_tensor(
+                    out=z[:],
+                    in0=acc_b[k][:],
+                    scalar=bias_col(TB, hq),
+                    in1=v1[k][:],
+                    op0=ALU.add,
+                    op1=ALU.add,
+                )
                 ff2 = work.tile([P, 512], F32, name="ff2", tag="ff2")
                 nc.scalar.activation(
                     out=ff2[:], in_=acc_2[k][:], func=ACT.Tanh, bias=bias_col(FF2, hq), scale=1.0
                 )
                 gate[k] = work.tile([P, 512], F32, name="gate", tag="gate")
                 nc.scalar.activation(
-                    out=gate[k][:], in_=z[:], func=ACT.Sigmoid, bias=bias_col(TB, hq), scale=1.0
+                    out=gate[k][:], in_=z[:], func=ACT.Sigmoid
                 )
             if 2 <= i <= n_u + 1:
                 k = i - 2

@@ -37,10 +37,9 @@ def tile_cfccell_pa_kernel(
         keep = ctx.enter_context(tc.tile_pool(name="keep", bufs=1))
         raw = ctx.enter_context(tc.tile_pool(name="raw", bufs=5))
         grp = ctx.enter_context(tc.tile_pool(name="grp", bufs=6))
-        thp = ctx.enter_context(tc.tile_pool(name="thp", bufs=2))
-        work = ctx.enter_context(tc.tile_pool(name="work", bufs=3))
+        thp = ctx.enter_context(tc.tile_pool(name="thp", bufs=3))
+        work = ctx.enter_context(tc.tile_pool(name="work", bufs=4))
         psum = ctx.enter_context(tc.psum_pool(name="psum", bufs=8))
-        ctx.enter_context(tc.manual_schedule())
 
         bias_rows = keep.tile([P, P], BF16, name="bias_rows")
         nc.vector.memset(bias_rows[:], 0.0)

@@ -16,11 +16,11 @@ TOK = 1024
 U_DIM = 1024
 V_DIM = 1024
 H_DIM = 512
+WIDE = 512
+PASSES = 2
 FLOPS = 2 * TOK * U_DIM * V_DIM + 4 * 2 * TOK * V_DIM * H_DIM
 
 FF1, FF2, TA, TB = 0, 1, 2, 3
-TRICK = True
-GD = False
 
 
 def tile_cfccell_pa_kernel(
@@ -57,10 +57,15 @@ def tile_cfccell_pa_kernel(
         make_identity(nc, ident_b[:])
         ident_f = keep.tile([P, P], F32, name="ident_f")
         make_identity(nc, ident_f[:])
+        ts_rows = keep.tile([P, TOK], BF16, name="ts_rows")
+        nc.gpsimd.memset(ts_rows[:], 0.0)
+        ones = keep.tile([P, P], BF16, name="ones")
+        nc.gpsimd.memset(ones[:], 1.0)
+        nc.scalar.dma_start(out=ts_rows[0:1, :], in_=ts_row.rearrange("(o t) -> o t", o=1))
 
         w1_raw = []
-        for g in range(2):
-            t_raw = raw.tile([P, 4, 1024], BF16, name="w1_raw%d" % g, tag="raw")
+        for g in range(PASSES):
+            t_raw = raw.tile([P, 4, V_DIM], BF16, name="w1_raw%d" % g, tag="raw")
             for u in range(2):
                 r0 = 512 * g + 256 * u
                 nc.sync.dma_start(
@@ -70,18 +75,18 @@ def tile_cfccell_pa_kernel(
             w1_raw.append(t_raw)
         h1_raw = []
         for n in range(2):
-            t_raw = raw.tile([P, 4, 1024], BF16, name="h1_raw%d" % n, tag="raw")
+            t_raw = raw.tile([P, 4, U_DIM], BF16, name="h1_raw%d" % n, tag="raw")
             nc.sync.dma_start(
                 out=t_raw[:],
-                in_=h1f[512 * n : 512 * n + 512, :].rearrange("(t p) u -> p t u", p=P),
+                in_=h1f[WIDE * n : WIDE * n + WIDE, :].rearrange("(t p) u -> p t u", p=P),
             )
             h1_raw.append(t_raw)
         ts_b = keep.tile([P, TOK], BF16, name="ts_b")
         hd_raw = {}
 
         def load_head(h):
-            t_raw = raw.tile([P, 2, 4, 512], BF16, name="hd_raw%d" % h, tag="raw")
-            for g in range(2):
+            t_raw = raw.tile([P, PASSES, 4, H_DIM], BF16, name="hd_raw%d" % h, tag="raw")
+            for g in range(PASSES):
                 nc.sync.dma_start(
                     out=t_raw[:, g, :, :],
                     in_=head_w[h][512 * g : 512 * g + 512, :].rearrange("(t p) n -> p t n", p=P),
@@ -91,39 +96,38 @@ def tile_cfccell_pa_kernel(
         load_head(FF1)
         load_head(TA)
         load_head(TB)
-        nc.sync.dma_start(out=ts_b[:], in_=ts_row.partition_broadcast(P))
         load_head(FF2)
 
         grouped = {}
         quant = {}
 
-        def regroup(eng, key, src):
-            g_t = grp.tile([P, 2048], BF16, name="g_%s_%d%d" % key, tag="grp", align_bytes=64)
+        def regroup(on_scalar, key, src):
+            g_t = grp.tile([P, 4 * WIDE], BF16, name="g_%s_%d%d" % key, tag="grp", align_bytes=64)
             dst = g_t[:].rearrange("p (c i t) -> p c t i", i=4, t=4)
             s_v = src.rearrange("p t (c i) -> p c t i", i=4)
-            if eng == "S":
+            if on_scalar:
                 nc.scalar.copy(out=dst, in_=s_v)
             else:
                 nc.vector.tensor_copy(out=dst, in_=s_v)
             grouped[key] = g_t
 
-        def r_w1(eng, g, cc):
-            regroup(eng, ("w", g, cc), w1_raw[g][:, :, 512 * cc : 512 * cc + 512])
+        def regroup_w1(on_scalar, g, half):
+            regroup(on_scalar, ("w", g, half), w1_raw[g][:, :, WIDE * half : WIDE * half + WIDE])
 
-        def r_hd(eng, h, g):
-            regroup(eng, ("h", h, g), hd_raw[h][:, g, :, :])
+        def regroup_head(on_scalar, h, g):
+            regroup(on_scalar, ("h", h, g), hd_raw[h][:, g, :, :])
 
-        def q(key):
-            codes = keep.tile([P, 512], U32, name="c_%s_%d%d" % key, align_bytes=64)
-            scales = keep.tile([P, 512], U8, name="s_%s_%d%d" % key, align_bytes=64)
+        def quantise(key):
+            codes = keep.tile([P, WIDE], U32, name="c_%s_%d%d" % key, align_bytes=64)
+            scales = keep.tile([P, WIDE], U8, name="s_%s_%d%d" % key, align_bytes=64)
             nc.vector.quantize_mx(
                 out=codes[:].bitcast(FP8X4), scales=scales[:], in_=grouped[key][:]
             )
             quant[key] = (codes, scales)
 
         def mx_group(stat, cols, mov):
-            acc = psum.tile([P, 512], F32, name="acc", tag="bank")
-            for g in range(2):
+            acc = psum.tile([P, WIDE], F32, name="acc", tag="bank")
+            for g in range(PASSES):
                 nc.tensor.matmul_mx(
                     out=acc[:],
                     lhsT=quant[stat[g]][0][:, cols].bitcast(FP8X4),
@@ -131,42 +135,40 @@ def tile_cfccell_pa_kernel(
                     rhs=quant[mov[g]][0][:].bitcast(FP8X4),
                     rhs_scale=quant[mov[g]][1][:],
                     start=(g == 0),
-                    stop=(g == 1),
+                    stop=(g == PASSES - 1),
                 )
             return acc
 
         def h1_transposes(n):
             banks = {}
-            for g in range(2):
-                for hh in range(2):
+            for g in range(PASSES):
+                for pair in range(2):
                     bank = psum.tile([P, 2, 256], F32, name="h1t", tag="bank")
                     for u in range(2):
                         for j in range(2):
                             c0 = 256 * g + 128 * u
                             nc.tensor.transpose(
                                 bank[:, u, 128 * j : 128 * j + 128],
-                                h1_raw[n][:, 2 * hh + j, :].bitcast(F32)[:, c0 : c0 + 128],
+                                h1_raw[n][:, 2 * pair + j, :].bitcast(F32)[:, c0 : c0 + 128],
                                 ident_f[:],
                             )
-                    banks[(g, hh)] = bank
+                    banks[(g, pair)] = bank
             return banks
 
-        def h1_out(eng, n, g, banks):
-            hg = grp.tile([P, 2048], BF16, name="g_a_%d%d" % (g, n), tag="grp", align_bytes=64)
+        def h1_out(n, g, banks):
+            hg = grp.tile([P, 4 * WIDE], BF16, name="g_a_%d%d" % (g, n), tag="grp", align_bytes=64)
             hgw = hg[:].bitcast(F32).rearrange("p (r u) -> p r u", u=2)
-            for hh in range(2):
-                dst = hgw[:, 256 * hh : 256 * hh + 256, :]
-                s_v = banks[(g, hh)][:].rearrange("p u r -> p r u")
-                if eng == "S":
-                    nc.scalar.copy(out=dst, in_=s_v)
-                else:
-                    nc.vector.tensor_copy(out=dst, in_=s_v)
+            for pair in range(2):
+                nc.scalar.copy(
+                    out=hgw[:, 256 * pair : 256 * pair + 256, :],
+                    in_=banks[(g, pair)][:].rearrange("p u r -> p r u"),
+                )
             grouped[("a", g, n)] = hg
 
         tanh_x = {}
 
         def stage1(n, gv):
-            th = thp.tile([P, 4, 512], F32, name="th", tag="th")
+            th = thp.tile([P, 4, WIDE], F32, name="th", tag="th")
             for t in range(4):
                 m = 4 * gv + t
                 acc = mx_group(
@@ -180,7 +182,7 @@ def tile_cfccell_pa_kernel(
             tanh_x[(gv, n)] = th
 
         def x_regroup(gv, n):
-            xg = grp.tile([P, 2048], BF16, name="g_x_%d%d" % (gv, n), tag="grp", align_bytes=64)
+            xg = grp.tile([P, 4 * WIDE], BF16, name="g_x_%d%d" % (gv, n), tag="grp", align_bytes=64)
             nc.vector.tensor_scalar_mul(
                 out=xg[:].rearrange("p (r i t) -> p r t i", i=4, t=4),
                 in0=tanh_x[(gv, n)][:].rearrange("p t (r i) -> p r t i", i=4),
@@ -200,66 +202,74 @@ def tile_cfccell_pa_kernel(
             c = 8 + 4 * h + hq
             return bias_t[:, c : c + 1]
 
-        r_w1("V", 0, 0)
-        r_w1("S", 0, 1)
+        regroup_w1(False, 0, 0)
+        regroup_w1(True, 0, 1)
         pb = psum.tile([P, P], BF16, name="pb", tag="bank")
         nc.tensor.transpose(pb[:], bias_rows[:], ident_b[:])
         bias_t = keep.tile([P, 24], F32, name="bias_t")
         nc.vector.tensor_copy(out=bias_t[:], in_=pb[:, 0:24])
         b1s = keep.tile([P, 8], F32, name="b1s")
         nc.vector.tensor_scalar_mul(out=b1s[:], in0=bias_t[:, 0:8], scalar1=0.666)
-        r_w1("V", 1, 0)
-        r_w1("S", 1, 1)
-        q(("w", 0, 0))
-        q(("w", 1, 0))
-        q(("w", 0, 1))
-        q(("w", 1, 1))
+        regroup_w1(False, 1, 0)
+        regroup_w1(True, 1, 1)
+        quantise(("w", 0, 0))
+        quantise(("w", 1, 0))
+        quantise(("w", 0, 1))
+        quantise(("w", 1, 1))
+        for n in range(2):
+            ts_acc = psum.tile([P, WIDE], F32, name="ts_acc", tag="bank")
+            nc.tensor.matmul(
+                out=ts_acc[:], lhsT=ones[:], rhs=ts_rows[:, WIDE * n : WIDE * n + WIDE],
+                start=True, stop=True,
+            )
+            nc.vector.tensor_copy(out=ts_b[:, WIDE * n : WIDE * n + WIDE], in_=ts_acc[:])
         t0 = h1_transposes(0)
         t1 = h1_transposes(1)
-        h1_out("S", 0, 0, t0)
-        h1_out("S", 0, 1, t0)
-        q(("a", 0, 0))
-        q(("a", 1, 0))
-        h1_out("S", 1, 0, t1)
-        h1_out("S", 1, 1, t1)
+        h1_out(0, 0, t0)
+        h1_out(0, 1, t0)
+        quantise(("a", 0, 0))
+        quantise(("a", 1, 0))
+        h1_out(1, 0, t1)
+        h1_out(1, 1, t1)
 
         stage1(0, 0)
         stage1(0, 1)
-        q(("a", 0, 1))
-        q(("a", 1, 1))
-        r_hd("V", FF1, 0)
+        quantise(("a", 0, 1))
+        quantise(("a", 1, 1))
+        regroup_head(False, FF1, 0)
         x_regroup(0, 0)
         stage1(1, 0)
-        r_hd("V", FF1, 1)
-        q(("x", 0, 0))
+        regroup_head(False, FF1, 1)
+        quantise(("x", 0, 0))
         x_regroup(1, 0)
         stage1(1, 1)
-        q(("h", FF1, 0))
-        r_hd("V", TA, 0)
-        q(("x", 1, 0))
-        q(("h", FF1, 1))
-        r_hd("S", TA, 1)
-        r_hd("S", TB, 0)
-        r_hd("S", TB, 1)
+        quantise(("h", FF1, 0))
+        regroup_head(False, TA, 0)
+        quantise(("x", 1, 0))
+        quantise(("h", FF1, 1))
+        regroup_head(True, TA, 1)
+        regroup_head(True, TB, 0)
+        regroup_head(True, TB, 1)
         x_regroup(0, 1)
-        q(("h", TA, 0))
-        q(("x", 0, 1))
+        quantise(("h", TA, 0))
+        quantise(("x", 0, 1))
         x_regroup(1, 1)
-        q(("h", TA, 1))
-        q(("x", 1, 1))
+        quantise(("h", TA, 1))
+        quantise(("x", 1, 1))
 
         units = [(hq, n) for n in range(2) for hq in range(4)]
         n_u = len(units)
+
         ff1 = {}
         v1 = {}
         acc_f = {}
         acc_a = {}
-        late = {
-            1: [("S", FF2, 0), ("q", TB, 0)],
-            2: [("V", FF2, 1)],
-            3: [("q", TB, 1)],
-            5: [("q", FF2, 1)],
-            6: [("q", FF2, 0)],
+        weight_steps = {
+            1: [("scalar", FF2, 0), ("quantise", TB, 0)],
+            2: [("vector", FF2, 1)],
+            3: [("quantise", TB, 1)],
+            5: [("quantise", FF2, 1)],
+            6: [("quantise", FF2, 0)],
         }
         for i in range(n_u + 1):
             if i < n_u:
@@ -268,30 +278,30 @@ def tile_cfccell_pa_kernel(
             if i >= 1:
                 k = i - 1
                 hq, n = units[k]
-                ff1[k] = keep.tile([P, 512], F32, name="ff1_%d" % k)
+                ff1[k] = keep.tile([P, WIDE], F32, name="ff1_%d" % k)
                 nc.scalar.activation(
                     out=ff1[k][:], in_=acc_f[k][:], func=ACT.Tanh, bias=bias_col(FF1, hq), scale=1.0
                 )
-                v1[k] = keep.tile([P, 512], F32, name="v1_%d" % k)
+                v1[k] = keep.tile([P, WIDE], F32, name="v1_%d" % k)
                 nc.vector.scalar_tensor_tensor(
                     out=v1[k][:],
                     in0=acc_a[k][:],
                     scalar=bias_col(TA, hq),
-                    in1=ts_b[:, 512 * n : 512 * n + 512],
+                    in1=ts_b[:, WIDE * n : WIDE * n + WIDE],
                     op0=ALU.add,
                     op1=ALU.mult,
                 )
-                for what, h, g in late.get(k, []):
-                    if what == "q":
-                        q(("h", h, g))
+                for what, h, g in weight_steps.get(k, []):
+                    if what == "quantise":
+                        quantise(("h", h, g))
                     else:
-                        r_hd(what, h, g)
+                        regroup_head(what == "scalar", h, g)
 
         acc_b = {}
         acc_2 = {}
         gate = {}
         dif = {}
-        res = {}
+        prod = {}
         for i in range(n_u + 3):
             if i < n_u:
                 acc_b[i] = head_group(TB, units[i])
@@ -301,21 +311,18 @@ def tile_cfccell_pa_kernel(
                 ot = psum.tile([P, 4, P], F32, name="ot", tag="bank")
                 for tt in range(4):
                     cols = slice(128 * tt, 128 * tt + 128)
-                    if TRICK:
-                        nc.tensor.matmul(
-                            out=ot[:, tt, :], lhsT=ff1[k][:, cols], rhs=ident_f[:],
-                            is_transpose=True, start=True, stop=False,
-                        )
-                        nc.tensor.matmul(
-                            out=ot[:, tt, :], lhsT=res[k][:, cols], rhs=ident_f[:],
-                            is_transpose=True, start=False, stop=True,
-                        )
-                    else:
-                        nc.tensor.transpose(ot[:, tt, :], res[k][:, cols], ident_f[:])
+                    nc.tensor.matmul(
+                        out=ot[:, tt, :], lhsT=ff1[k][:, cols], rhs=ident_f[:],
+                        is_transpose=True, start=True, stop=False,
+                    )
+                    nc.tensor.matmul(
+                        out=ot[:, tt, :], lhsT=prod[k][:, cols], rhs=ident_f[:],
+                        is_transpose=True, start=False, stop=True,
+                    )
             if 1 <= i <= n_u:
                 k = i - 1
                 hq, n = units[k]
-                z = work.tile([P, 512], F32, name="z", tag="z")
+                z = work.tile([P, WIDE], F32, name="z", tag="z")
                 nc.vector.scalar_tensor_tensor(
                     out=z[:],
                     in0=acc_b[k][:],
@@ -324,37 +331,27 @@ def tile_cfccell_pa_kernel(
                     op0=ALU.add,
                     op1=ALU.add,
                 )
-                ff2 = work.tile([P, 512], F32, name="ff2", tag="ff2")
+                ff2 = work.tile([P, WIDE], F32, name="ff2", tag="ff2")
                 nc.scalar.activation(
                     out=ff2[:], in_=acc_2[k][:], func=ACT.Tanh, bias=bias_col(FF2, hq), scale=1.0
                 )
-                gate[k] = work.tile([P, 512], F32, name="gate", tag="gate")
-                nc.scalar.activation(
-                    out=gate[k][:], in_=z[:], func=ACT.Sigmoid
-                )
+                gate[k] = work.tile([P, WIDE], F32, name="gate", tag="gate")
+                nc.scalar.activation(out=gate[k][:], in_=z[:], func=ACT.Sigmoid)
             if 2 <= i <= n_u + 1:
                 k = i - 2
-                e = work.tile([P, 512], F32, name="e", tag="e")
-                nc.vector.tensor_mul(out=e[:], in0=gate[k][:], in1=dif[k][:])
-                if TRICK:
-                    res[k] = e
-                else:
-                    res[k] = work.tile([P, 512], F32, name="o", tag="o")
-                    nc.vector.tensor_add(out=res[k][:], in0=e[:], in1=ff1[k][:])
+                prod[k] = work.tile([P, WIDE], F32, name="e", tag="e")
+                nc.vector.tensor_mul(out=prod[k][:], in0=gate[k][:], in1=dif[k][:])
             if 1 <= i <= n_u:
                 k = i - 1
-                dif[k] = work.tile([P, 512], F32, name="dif", tag="dif")
-                if GD:
-                    nc.gpsimd.tensor_tensor(out=dif[k][:], in0=ff2[:], in1=ff1[k][:], op=ALU.subtract)
-                else:
-                    nc.vector.tensor_sub(out=dif[k][:], in0=ff2[:], in1=ff1[k][:])
+                dif[k] = work.tile([P, WIDE], F32, name="dif", tag="dif")
+                nc.vector.tensor_sub(out=dif[k][:], in0=ff2[:], in1=ff1[k][:])
             if 3 <= i:
                 k = i - 3
                 hq, n = units[k]
                 ost = work.tile([P, 4, P], F32, name="ost", tag="ost")
                 nc.scalar.copy(out=ost[:], in_=ot[:])
                 nc.sync.dma_start(
-                    out=outf[512 * n : 512 * n + 512, 128 * hq : 128 * hq + 128].rearrange(
+                    out=outf[WIDE * n : WIDE * n + WIDE, 128 * hq : 128 * hq + 128].rearrange(
                         "(t p) h -> p t h", p=P
                     ),
                     in_=ost[:],

@@ -41,6 +41,11 @@ def tile_cfccell_pa_kernel(
         work = ctx.enter_context(tc.tile_pool(name="work", bufs=4))
         psum = ctx.enter_context(tc.psum_pool(name="psum", bufs=8))
 
+        ts_rows = keep.tile([P, TOK], BF16, name="ts_rows")
+        nc.vector.memset(ts_rows[:], 0.0)
+        nc.scalar.dma_start(out=ts_rows[0:1, :], in_=ts_row.rearrange("(o t) -> o t", o=1))
+        ones = keep.tile([P, P], BF16, name="ones")
+        nc.vector.memset(ones[:], 1.0)
         bias_rows = keep.tile([P, P], BF16, name="bias_rows")
         nc.vector.memset(bias_rows[:], 0.0)
         nc.scalar.dma_start(out=bias_rows[0:8, :], in_=b1.rearrange("(r c) -> r c", c=P))
@@ -57,12 +62,6 @@ def tile_cfccell_pa_kernel(
         make_identity(nc, ident_b[:])
         ident_f = keep.tile([P, P], F32, name="ident_f")
         make_identity(nc, ident_f[:])
-        ts_rows = keep.tile([P, TOK], BF16, name="ts_rows")
-        nc.gpsimd.memset(ts_rows[:], 0.0)
-        ones = keep.tile([P, P], BF16, name="ones")
-        nc.gpsimd.memset(ones[:], 1.0)
-        nc.scalar.dma_start(out=ts_rows[0:1, :], in_=ts_row.rearrange("(o t) -> o t", o=1))
-
         w1_raw = []
         for g in range(PASSES):
             t_raw = raw.tile([P, 4, V_DIM], BF16, name="w1_raw%d" % g, tag="raw")
@@ -210,12 +209,6 @@ def tile_cfccell_pa_kernel(
         nc.vector.tensor_copy(out=bias_t[:], in_=pb[:, 0:24])
         b1s = keep.tile([P, 8], F32, name="b1s")
         nc.vector.tensor_scalar_mul(out=b1s[:], in0=bias_t[:, 0:8], scalar1=0.666)
-        regroup_w1(False, 1, 0)
-        regroup_w1(True, 1, 1)
-        quantise(("w", 0, 0))
-        quantise(("w", 1, 0))
-        quantise(("w", 0, 1))
-        quantise(("w", 1, 1))
         for n in range(2):
             ts_acc = psum.tile([P, WIDE], F32, name="ts_acc", tag="bank")
             nc.tensor.matmul(
@@ -223,6 +216,12 @@ def tile_cfccell_pa_kernel(
                 start=True, stop=True,
             )
             nc.vector.tensor_copy(out=ts_b[:, WIDE * n : WIDE * n + WIDE], in_=ts_acc[:])
+        regroup_w1(False, 1, 0)
+        regroup_w1(True, 1, 1)
+        quantise(("w", 0, 0))
+        quantise(("w", 1, 0))
+        quantise(("w", 0, 1))
+        quantise(("w", 1, 1))
         t0 = h1_transposes(0)
         t1 = h1_transposes(1)
         h1_out(0, 0, t0)

@@ -35,88 +35,108 @@ def tile_cfccell_pa_kernel(
 
     with ExitStack() as ctx:
         keep = ctx.enter_context(tc.tile_pool(name="keep", bufs=1))
-        raw = ctx.enter_context(tc.tile_pool(name="raw", bufs=5))
+        raw = ctx.enter_context(tc.tile_pool(name="raw", bufs=12))
         grp = ctx.enter_context(tc.tile_pool(name="grp", bufs=6))
         thp = ctx.enter_context(tc.tile_pool(name="thp", bufs=3))
-        work = ctx.enter_context(tc.tile_pool(name="work", bufs=4))
+        work = ctx.enter_context(tc.tile_pool(name="work", bufs=3))
+        stp = ctx.enter_context(tc.tile_pool(name="stp", bufs=4))
         psum = ctx.enter_context(tc.psum_pool(name="psum", bufs=8))
 
-        ts_rows = keep.tile([P, TOK], BF16, name="ts_rows")
-        nc.vector.memset(ts_rows[:], 0.0)
-        nc.scalar.dma_start(out=ts_rows[0:1, :], in_=ts_row.rearrange("(o t) -> o t", o=1))
-        ones = keep.tile([P, P], BF16, name="ones")
-        nc.vector.memset(ones[:], 1.0)
-        bias_rows = keep.tile([P, P], BF16, name="bias_rows")
-        nc.vector.memset(bias_rows[:], 0.0)
-        nc.scalar.dma_start(out=bias_rows[0:8, :], in_=b1.rearrange("(r c) -> r c", c=P))
-        for h in range(4):
-            nc.scalar.dma_start(
-                out=bias_rows[8 + 4 * h : 12 + 4 * h, :],
-                in_=head_b[h].rearrange("(r c) -> r c", c=P),
-            )
         warm = keep.tile([P, 1], F32, name="warm")
         nc.vector.memset(warm[:], 0.0)
         warm_out = keep.tile([P, 1], F32, name="warm_out")
         nc.scalar.activation(out=warm_out[:], in_=warm[:], func=ACT.Sigmoid)
-        ident_b = keep.tile([P, P], BF16, name="ident_b")
-        make_identity(nc, ident_b[:])
+        ts_rows = keep.tile([P, TOK], BF16, name="ts_rows")
+        nc.vector.memset(ts_rows[:], 0.0)
+        ones = keep.tile([P, P], BF16, name="ones")
+        nc.vector.memset(ones[:], 1.0)
+        bias_rows = keep.tile([P, P], BF16, name="bias_rows")
+        nc.vector.memset(bias_rows[:], 0.0)
         ident_f = keep.tile([P, P], F32, name="ident_f")
         make_identity(nc, ident_f[:])
-        w1_raw = []
-        for g in range(PASSES):
-            t_raw = raw.tile([P, 4, V_DIM], BF16, name="w1_raw%d" % g, tag="raw")
+        ident_b = keep.tile([P, P], BF16, name="ident_b")
+        make_identity(nc, ident_b[:])
+        ts_b = keep.tile([P, TOK], BF16, name="ts_b")
+        ctx.enter_context(tc.manual_schedule())
+
+        w1_raw = {}
+        h1_raw = {}
+        hd_raw = {}
+
+        def load_w1(g, half):
+            t_raw = raw.tile([P, 4, WIDE], BF16, name="w1_raw%d%d" % (g, half), tag="raw")
             for u in range(2):
                 r0 = 512 * g + 256 * u
                 nc.sync.dma_start(
                     out=t_raw[:, 2 * u : 2 * u + 2, :],
-                    in_=W1[r0 : r0 + 256, :].rearrange("(q e) c -> q e c", e=2),
+                    in_=W1[r0 : r0 + 256, WIDE * half : WIDE * half + WIDE].rearrange(
+                        "(q e) c -> q e c", e=2
+                    ),
                 )
-            w1_raw.append(t_raw)
-        h1_raw = []
-        for n in range(2):
-            t_raw = raw.tile([P, 4, U_DIM], BF16, name="h1_raw%d" % n, tag="raw")
+            w1_raw[(g, half)] = t_raw
+
+        def load_h1(n, pair):
+            t_raw = raw.tile([P, 2, U_DIM], BF16, name="h1_raw%d%d" % (n, pair), tag="raw")
+            r0 = WIDE * n + 256 * pair
             nc.sync.dma_start(
-                out=t_raw[:],
-                in_=h1f[WIDE * n : WIDE * n + WIDE, :].rearrange("(t p) u -> p t u", p=P),
+                out=t_raw[:], in_=h1f[r0 : r0 + 256, :].rearrange("(t p) u -> p t u", p=P)
             )
-            h1_raw.append(t_raw)
-        ts_b = keep.tile([P, TOK], BF16, name="ts_b")
-        hd_raw = {}
+            h1_raw[(n, pair)] = t_raw
 
         def load_head(h):
-            t_raw = raw.tile([P, PASSES, 4, H_DIM], BF16, name="hd_raw%d" % h, tag="raw")
             for g in range(PASSES):
+                t_raw = raw.tile([P, 4, H_DIM], BF16, name="hd_raw%d%d" % (h, g), tag="raw")
                 nc.sync.dma_start(
-                    out=t_raw[:, g, :, :],
+                    out=t_raw[:],
                     in_=head_w[h][512 * g : 512 * g + 512, :].rearrange("(t p) n -> p t n", p=P),
                 )
-            hd_raw[h] = t_raw
+                hd_raw[(h, g)] = t_raw
 
+        load_w1(0, 0)
+        load_h1(0, 0)
+        load_w1(1, 0)
+        load_h1(0, 1)
+        nc.sync.dma_start(out=bias_rows[0:8, :], in_=b1.rearrange("(r c) -> r c", c=P))
+        for h in range(4):
+            nc.sync.dma_start(
+                out=bias_rows[8 + 4 * h : 12 + 4 * h, :],
+                in_=head_b[h].rearrange("(r c) -> r c", c=P),
+            )
+        nc.sync.dma_start(out=ts_rows[0:1, :], in_=ts_row.rearrange("(o t) -> o t", o=1))
+        load_w1(0, 1)
+        load_w1(1, 1)
+        load_h1(1, 0)
+        load_h1(1, 1)
         load_head(FF1)
         load_head(TA)
-        load_head(TB)
-        load_head(FF2)
 
         grouped = {}
         quant = {}
 
-        def regroup(on_scalar, key, src):
-            g_t = grp.tile([P, 4 * WIDE], BF16, name="g_%s_%d%d" % key, tag="grp", align_bytes=64)
-            dst = g_t[:].rearrange("p (c i t) -> p c t i", i=4, t=4)
-            s_v = src.rearrange("p t (c i) -> p c t i", i=4)
+        def regroup_half(on_scalar, key, part):
+            if key not in grouped:
+                grouped[key] = grp.tile(
+                    [P, 4 * WIDE], BF16, name="g_%s_%d%d" % key, tag="grp", align_bytes=64
+                )
+            src = w1_raw[key[1:]] if key[0] == "w" else hd_raw[key[1:]]
+            dst = grouped[key][:, 1024 * part : 1024 * part + 1024].rearrange(
+                "p (c i t) -> p c t i", i=4, t=4
+            )
+            s_v = src[:, :, 256 * part : 256 * part + 256].rearrange("p t (c i) -> p c t i", i=4)
             if on_scalar:
                 nc.scalar.copy(out=dst, in_=s_v)
             else:
                 nc.vector.tensor_copy(out=dst, in_=s_v)
-            grouped[key] = g_t
 
-        def regroup_w1(on_scalar, g, half):
-            regroup(on_scalar, ("w", g, half), w1_raw[g][:, :, WIDE * half : WIDE * half + WIDE])
+        def split(*key):
+            regroup_half(True, key, 0)
+            regroup_half(False, key, 1)
 
-        def regroup_head(on_scalar, h, g):
-            regroup(on_scalar, ("h", h, g), hd_raw[h][:, g, :, :])
+        def vector_all(*key):
+            regroup_half(False, key, 0)
+            regroup_half(False, key, 1)
 
-        def quantise(key):
+        def quantise(*key):
             codes = keep.tile([P, WIDE], U32, name="c_%s_%d%d" % key, align_bytes=64)
             scales = keep.tile([P, WIDE], U8, name="s_%s_%d%d" % key, align_bytes=64)
             nc.vector.quantize_mx(
@@ -138,45 +158,52 @@ def tile_cfccell_pa_kernel(
                 )
             return acc
 
-        def h1_transposes(n):
-            banks = {}
-            for g in range(PASSES):
-                for pair in range(2):
-                    bank = psum.tile([P, 2, 256], F32, name="h1t", tag="bank")
-                    for u in range(2):
-                        for j in range(2):
-                            c0 = 256 * g + 128 * u
-                            nc.tensor.transpose(
-                                bank[:, u, 128 * j : 128 * j + 128],
-                                h1_raw[n][:, 2 * pair + j, :].bitcast(F32)[:, c0 : c0 + 128],
-                                ident_f[:],
-                            )
-                    banks[(g, pair)] = bank
-            return banks
+        h1_banks = {}
 
-        def h1_out(n, g, banks):
-            hg = grp.tile([P, 4 * WIDE], BF16, name="g_a_%d%d" % (g, n), tag="grp", align_bytes=64)
-            hgw = hg[:].bitcast(F32).rearrange("p (r u) -> p r u", u=2)
-            for pair in range(2):
+        def h1_transposes(n, pair):
+            for g in range(PASSES):
+                bank = psum.tile([P, 2, 256], F32, name="h1t", tag="bank")
+                for u in range(2):
+                    for j in range(2):
+                        c0 = 256 * g + 128 * u
+                        nc.tensor.transpose(
+                            bank[:, u, 128 * j : 128 * j + 128],
+                            h1_raw[(n, pair)][:, j, :].bitcast(F32)[:, c0 : c0 + 128],
+                            ident_f[:],
+                        )
+                h1_banks[(n, g, pair)] = bank
+
+        def h1_out(n, pair):
+            for g in range(PASSES):
+                key = ("a", g, n)
+                if key not in grouped:
+                    grouped[key] = grp.tile(
+                        [P, 4 * WIDE], BF16, name="g_%s_%d%d" % key, tag="grp", align_bytes=64
+                    )
+                hgw = grouped[key][:].bitcast(F32).rearrange("p (r u) -> p r u", u=2)
                 nc.scalar.copy(
                     out=hgw[:, 256 * pair : 256 * pair + 256, :],
-                    in_=banks[(g, pair)][:].rearrange("p u r -> p r u"),
+                    in_=h1_banks[(n, g, pair)][:].rearrange("p u r -> p r u"),
                 )
-            grouped[("a", g, n)] = hg
 
+        acc_x = {}
         tanh_x = {}
 
-        def stage1(n, gv):
-            th = thp.tile([P, 4, WIDE], F32, name="th", tag="th")
+        def stage1_mm(n, gv):
             for t in range(4):
-                m = 4 * gv + t
-                acc = mx_group(
+                acc_x[(n, gv, t)] = mx_group(
                     [("w", 0, gv), ("w", 1, gv)],
                     slice(128 * t, 128 * t + 128),
                     [("a", 0, n), ("a", 1, n)],
                 )
+
+        def stage1_tanh(n, gv):
+            th = thp.tile([P, 4, WIDE], F32, name="th", tag="th")
+            for t in range(4):
+                m = 4 * gv + t
                 nc.scalar.activation(
-                    out=th[:, t, :], in_=acc[:], func=ACT.Tanh, bias=b1s[:, m : m + 1], scale=0.666
+                    out=th[:, t, :], in_=acc_x[(n, gv, t)][:], func=ACT.Tanh,
+                    bias=b1s[:, m : m + 1], scale=0.666,
                 )
             tanh_x[(gv, n)] = th
 
@@ -201,60 +228,66 @@ def tile_cfccell_pa_kernel(
             c = 8 + 4 * h + hq
             return bias_t[:, c : c + 1]
 
-        regroup_w1(False, 0, 0)
-        regroup_w1(True, 0, 1)
+        h1_transposes(0, 0)
+        split("w", 0, 0)
+        vector_all("w", 1, 0)
+        quantise("w", 0, 0)
+        h1_out(0, 0)
+        h1_transposes(0, 1)
+        quantise("w", 1, 0)
+        h1_out(0, 1)
+        quantise("a", 0, 0)
+        quantise("a", 1, 0)
+        split("w", 0, 1)
+        split("w", 1, 1)
         pb = psum.tile([P, P], BF16, name="pb", tag="bank")
         nc.tensor.transpose(pb[:], bias_rows[:], ident_b[:])
         bias_t = keep.tile([P, 24], F32, name="bias_t")
         nc.vector.tensor_copy(out=bias_t[:], in_=pb[:, 0:24])
         b1s = keep.tile([P, 8], F32, name="b1s")
         nc.vector.tensor_scalar_mul(out=b1s[:], in0=bias_t[:, 0:8], scalar1=0.666)
+        stage1_mm(0, 0)
+        stage1_tanh(0, 0)
+        quantise("w", 0, 1)
+        quantise("w", 1, 1)
+        load_head(TB)
+        load_head(FF2)
+        h1_transposes(1, 0)
+        h1_transposes(1, 1)
+        stage1_mm(0, 1)
+        h1_out(1, 0)
+        h1_out(1, 1)
+        stage1_tanh(0, 1)
+        ts_acc = psum.tile([P, TOK], BF16, name="ts_acc", tag="bank")
         for n in range(2):
-            ts_acc = psum.tile([P, WIDE], F32, name="ts_acc", tag="bank")
             nc.tensor.matmul(
-                out=ts_acc[:], lhsT=ones[:], rhs=ts_rows[:, WIDE * n : WIDE * n + WIDE],
-                start=True, stop=True,
+                out=ts_acc[:, WIDE * n : WIDE * n + WIDE], lhsT=ones[:],
+                rhs=ts_rows[:, WIDE * n : WIDE * n + WIDE], start=True, stop=True,
             )
-            nc.vector.tensor_copy(out=ts_b[:, WIDE * n : WIDE * n + WIDE], in_=ts_acc[:])
-        regroup_w1(False, 1, 0)
-        regroup_w1(True, 1, 1)
-        quantise(("w", 0, 0))
-        quantise(("w", 1, 0))
-        quantise(("w", 0, 1))
-        quantise(("w", 1, 1))
-        t0 = h1_transposes(0)
-        t1 = h1_transposes(1)
-        h1_out(0, 0, t0)
-        h1_out(0, 1, t0)
-        quantise(("a", 0, 0))
-        quantise(("a", 1, 0))
-        h1_out(1, 0, t1)
-        h1_out(1, 1, t1)
-
-        stage1(0, 0)
-        stage1(0, 1)
-        quantise(("a", 0, 1))
-        quantise(("a", 1, 1))
-        regroup_head(False, FF1, 0)
+        vector_all("h", FF1, 0)
         x_regroup(0, 0)
-        stage1(1, 0)
-        regroup_head(False, FF1, 1)
-        quantise(("x", 0, 0))
+        quantise("a", 0, 1)
+        quantise("a", 1, 1)
+        quantise("h", FF1, 0)
+        quantise("x", 0, 0)
+        split("h", FF1, 1)
         x_regroup(1, 0)
-        stage1(1, 1)
-        quantise(("h", FF1, 0))
-        regroup_head(False, TA, 0)
-        quantise(("x", 1, 0))
-        quantise(("h", FF1, 1))
-        regroup_head(True, TA, 1)
-        regroup_head(True, TB, 0)
-        regroup_head(True, TB, 1)
+        quantise("h", FF1, 1)
+        quantise("x", 1, 0)
+        split("h", TA, 0)
+        split("h", TA, 1)
+        nc.scalar.copy(out=ts_b[:], in_=ts_acc[:])
+        for gv in range(2):
+            stage1_mm(1, gv)
+            stage1_tanh(1, gv)
+        quantise("h", TA, 0)
+        quantise("h", TA, 1)
         x_regroup(0, 1)
-        quantise(("h", TA, 0))
-        quantise(("x", 0, 1))
+        split("h", TB, 0)
+        quantise("x", 0, 1)
         x_regroup(1, 1)
-        quantise(("h", TA, 1))
-        quantise(("x", 1, 1))
+        split("h", TB, 1)
+        quantise("x", 1, 1)
 
         units = [(hq, n) for n in range(2) for hq in range(4)]
         n_u = len(units)
@@ -263,13 +296,6 @@ def tile_cfccell_pa_kernel(
         v1 = {}
         acc_f = {}
         acc_a = {}
-        weight_steps = {
-            1: [("scalar", FF2, 0), ("quantise", TB, 0)],
-            2: [("vector", FF2, 1)],
-            3: [("quantise", TB, 1)],
-            5: [("quantise", FF2, 1)],
-            6: [("quantise", FF2, 0)],
-        }
         for i in range(n_u + 1):
             if i < n_u:
                 acc_f[i] = head_group(FF1, units[i])
@@ -290,11 +316,17 @@ def tile_cfccell_pa_kernel(
                     op0=ALU.add,
                     op1=ALU.mult,
                 )
-                for what, h, g in weight_steps.get(k, []):
-                    if what == "quantise":
-                        quantise(("h", h, g))
-                    else:
-                        regroup_head(what == "scalar", h, g)
+            if i == 1:
+                split("h", FF2, 0)
+            if i == 2:
+                quantise("h", TB, 0)
+            if i == 3:
+                quantise("h", TB, 1)
+                split("h", FF2, 1)
+            if i == 4:
+                quantise("h", FF2, 0)
+            if i == 5:
+                quantise("h", FF2, 1)
 
         acc_b = {}
         acc_2 = {}
@@ -347,7 +379,7 @@ def tile_cfccell_pa_kernel(
             if 3 <= i:
                 k = i - 3
                 hq, n = units[k]
-                ost = work.tile([P, 4, P], F32, name="ost", tag="ost")
+                ost = stp.tile([P, 4, P], F32, name="ost", tag="ost")
                 nc.scalar.copy(out=ost[:], in_=ot[:])
                 nc.sync.dma_start(
                     out=outf[WIDE * n : WIDE * n + WIDE, 128 * hq : 128 * hq + 128].rearrange(

@@ -36,8 +36,8 @@ def tile_cfccell_pa_kernel(
     with ExitStack() as ctx:
         keep = ctx.enter_context(tc.tile_pool(name="keep", bufs=1))
         raw = ctx.enter_context(tc.tile_pool(name="raw", bufs=12))
-        grp = ctx.enter_context(tc.tile_pool(name="grp", bufs=6))
-        thp = ctx.enter_context(tc.tile_pool(name="thp", bufs=3))
+        grp = ctx.enter_context(tc.tile_pool(name="grp", bufs=5))
+        thp = ctx.enter_context(tc.tile_pool(name="thp", bufs=2))
         work = ctx.enter_context(tc.tile_pool(name="work", bufs=3))
         stp = ctx.enter_context(tc.tile_pool(name="stp", bufs=4))
         psum = ctx.enter_context(tc.psum_pool(name="psum", bufs=8))
@@ -113,46 +113,47 @@ def tile_cfccell_pa_kernel(
         grouped = {}
         quant = {}
 
-        def regroup_half(on_scalar, key, part):
+        def group_tile(key):
             if key not in grouped:
                 grouped[key] = grp.tile(
-                    [P, 4 * WIDE], BF16, name="g_%s_%d%d" % key, tag="grp", align_bytes=64
+                    [P, PASSES, 4 * WIDE], BF16, name="g_%s%d" % key, tag="grp", align_bytes=64
                 )
-            src = w1_raw[key[1:]] if key[0] == "w" else hd_raw[key[1:]]
-            dst = grouped[key][:, 1024 * part : 1024 * part + 1024].rearrange(
-                "p (c i t) -> p c t i", i=4, t=4
-            )
-            s_v = src[:, :, 256 * part : 256 * part + 256].rearrange("p t (c i) -> p c t i", i=4)
+            return grouped[key]
+
+        def regroup(on_scalar, key, g, c0, c1):
+            src = w1_raw[(g, key[1])] if key[0] == "w" else hd_raw[(key[1], g)]
+            dst = group_tile(key)[:, g, 4 * c0 : 4 * c1].rearrange("p (c i t) -> p c t i", i=4, t=4)
+            s_v = src[:, :, c0:c1].rearrange("p t (c i) -> p c t i", i=4)
             if on_scalar:
                 nc.scalar.copy(out=dst, in_=s_v)
             else:
                 nc.vector.tensor_copy(out=dst, in_=s_v)
 
-        def split(*key):
-            regroup_half(True, key, 0)
-            regroup_half(False, key, 1)
+        def split(key, g):
+            regroup(True, key, g, 0, WIDE // 2)
+            regroup(False, key, g, WIDE // 2, WIDE)
 
-        def vector_all(*key):
-            regroup_half(False, key, 0)
-            regroup_half(False, key, 1)
-
-        def quantise(*key):
-            codes = keep.tile([P, WIDE], U32, name="c_%s_%d%d" % key, align_bytes=64)
-            scales = keep.tile([P, WIDE], U8, name="s_%s_%d%d" % key, align_bytes=64)
+        def quantise(key):
+            codes = keep.tile([P, PASSES * WIDE], U32, name="c_%s%d" % key, align_bytes=64)
+            scales = keep.tile([P, PASSES * WIDE], U8, name="s_%s%d" % key, align_bytes=64)
             nc.vector.quantize_mx(
-                out=codes[:].bitcast(FP8X4), scales=scales[:], in_=grouped[key][:]
+                out=codes[:].bitcast(FP8X4),
+                scales=scales[:],
+                in_=grouped[key][:].rearrange("p g c -> p (g c)"),
             )
             quant[key] = (codes, scales)
 
-        def mx_group(stat, cols, mov):
+        def mx_group(stat, tile_no, mov):
             acc = psum.tile([P, WIDE], F32, name="acc", tag="bank")
             for g in range(PASSES):
+                s0 = WIDE * g + P * tile_no
+                m_cols = slice(WIDE * g, WIDE * g + WIDE)
                 nc.tensor.matmul_mx(
                     out=acc[:],
-                    lhsT=quant[stat[g]][0][:, cols].bitcast(FP8X4),
-                    lhsT_scale=quant[stat[g]][1][:, cols],
-                    rhs=quant[mov[g]][0][:].bitcast(FP8X4),
-                    rhs_scale=quant[mov[g]][1][:],
+                    lhsT=quant[stat][0][:, s0 : s0 + P].bitcast(FP8X4),
+                    lhsT_scale=quant[stat][1][:, s0 : s0 + P],
+                    rhs=quant[mov][0][:, m_cols].bitcast(FP8X4),
+                    rhs_scale=quant[mov][1][:, m_cols],
                     start=(g == 0),
                     stop=(g == PASSES - 1),
                 )
@@ -175,12 +176,7 @@ def tile_cfccell_pa_kernel(
 
         def h1_out(n, pair):
             for g in range(PASSES):
-                key = ("a", g, n)
-                if key not in grouped:
-                    grouped[key] = grp.tile(
-                        [P, 4 * WIDE], BF16, name="g_%s_%d%d" % key, tag="grp", align_bytes=64
-                    )
-                hgw = grouped[key][:].bitcast(F32).rearrange("p (r u) -> p r u", u=2)
+                hgw = group_tile(("a", n))[:, g, :].bitcast(F32).rearrange("p (r u) -> p r u", u=2)
                 nc.scalar.copy(
                     out=hgw[:, 256 * pair : 256 * pair + 256, :],
                     in_=h1_banks[(n, g, pair)][:].rearrange("p u r -> p r u"),
@@ -191,11 +187,7 @@ def tile_cfccell_pa_kernel(
 
         def stage1_mm(n, gv):
             for t in range(4):
-                acc_x[(n, gv, t)] = mx_group(
-                    [("w", 0, gv), ("w", 1, gv)],
-                    slice(128 * t, 128 * t + 128),
-                    [("a", 0, n), ("a", 1, n)],
-                )
+                acc_x[(n, gv, t)] = mx_group(("w", gv), t, ("a", n))
 
         def stage1_tanh(n, gv):
             th = thp.tile([P, 4, WIDE], F32, name="th", tag="th")
@@ -208,38 +200,30 @@ def tile_cfccell_pa_kernel(
             tanh_x[(gv, n)] = th
 
         def x_regroup(gv, n):
-            xg = grp.tile([P, 4 * WIDE], BF16, name="g_x_%d%d" % (gv, n), tag="grp", align_bytes=64)
             nc.vector.tensor_scalar_mul(
-                out=xg[:].rearrange("p (r i t) -> p r t i", i=4, t=4),
+                out=group_tile(("x", n))[:, gv, :].rearrange("p (r i t) -> p r t i", i=4, t=4),
                 in0=tanh_x[(gv, n)][:].rearrange("p t (r i) -> p r t i", i=4),
                 scalar1=1.7159,
             )
-            grouped[("x", gv, n)] = xg
 
         def head_group(h, unit):
             hq, n = unit
-            return mx_group(
-                [("h", h, 0), ("h", h, 1)],
-                slice(128 * hq, 128 * hq + 128),
-                [("x", 0, n), ("x", 1, n)],
-            )
+            return mx_group(("h", h), hq, ("x", n))
 
         def bias_col(h, hq):
             c = 8 + 4 * h + hq
             return bias_t[:, c : c + 1]
 
         h1_transposes(0, 0)
-        split("w", 0, 0)
-        vector_all("w", 1, 0)
-        quantise("w", 0, 0)
+        split(("w", 0), 0)
+        regroup(False, ("w", 0), 1, 0, WIDE)
         h1_out(0, 0)
         h1_transposes(0, 1)
-        quantise("w", 1, 0)
+        quantise(("w", 0))
         h1_out(0, 1)
-        quantise("a", 0, 0)
-        quantise("a", 1, 0)
-        split("w", 0, 1)
-        split("w", 1, 1)
+        quantise(("a", 0))
+        split(("w", 1), 0)
+        split(("w", 1), 1)
         pb = psum.tile([P, P], BF16, name="pb", tag="bank")
         nc.tensor.transpose(pb[:], bias_rows[:], ident_b[:])
         bias_t = keep.tile([P, 24], F32, name="bias_t")
@@ -248,8 +232,7 @@ def tile_cfccell_pa_kernel(
         nc.vector.tensor_scalar_mul(out=b1s[:], in0=bias_t[:, 0:8], scalar1=0.666)
         stage1_mm(0, 0)
         stage1_tanh(0, 0)
-        quantise("w", 0, 1)
-        quantise("w", 1, 1)
+        quantise(("w", 1))
         load_head(TB)
         load_head(FF2)
         h1_transposes(1, 0)
@@ -264,30 +247,25 @@ def tile_cfccell_pa_kernel(
                 out=ts_acc[:, WIDE * n : WIDE * n + WIDE], lhsT=ones[:],
                 rhs=ts_rows[:, WIDE * n : WIDE * n + WIDE], start=True, stop=True,
             )
-        vector_all("h", FF1, 0)
+        regroup(False, ("h", FF1), 0, 0, WIDE)
+        split(("h", FF1), 1)
         x_regroup(0, 0)
-        quantise("a", 0, 1)
-        quantise("a", 1, 1)
-        quantise("h", FF1, 0)
-        quantise("x", 0, 0)
-        split("h", FF1, 1)
+        quantise(("a", 1))
+        regroup(False, ("h", TA), 0, 0, WIDE)
         x_regroup(1, 0)
-        quantise("h", FF1, 1)
-        quantise("x", 1, 0)
-        split("h", TA, 0)
-        split("h", TA, 1)
-        nc.scalar.copy(out=ts_b[:], in_=ts_acc[:])
+        quantise(("h", FF1))
+        quantise(("x", 0))
+        regroup(True, ("h", TA), 1, 0, WIDE)
         for gv in range(2):
             stage1_mm(1, gv)
             stage1_tanh(1, gv)
-        quantise("h", TA, 0)
-        quantise("h", TA, 1)
+        nc.scalar.copy(out=ts_b[:], in_=ts_acc[:])
+        quantise(("h", TA))
+        regroup(False, ("h", TB), 0, 0, WIDE)
         x_regroup(0, 1)
-        split("h", TB, 0)
-        quantise("x", 0, 1)
+        regroup(True, ("h", TB), 1, 0, WIDE)
+        regroup(False, ("h", FF2), 0, 0, WIDE)
         x_regroup(1, 1)
-        split("h", TB, 1)
-        quantise("x", 1, 1)
 
         units = [(hq, n) for n in range(2) for hq in range(4)]
         n_u = len(units)
@@ -317,28 +295,24 @@ def tile_cfccell_pa_kernel(
                     op1=ALU.mult,
                 )
             if i == 1:
-                split("h", FF2, 0)
-            if i == 2:
-                quantise("h", TB, 0)
-            if i == 3:
-                quantise("h", TB, 1)
-                split("h", FF2, 1)
+                quantise(("x", 1))
+                regroup(True, ("h", FF2), 1, 0, WIDE)
             if i == 4:
-                quantise("h", FF2, 0)
+                quantise(("h", TB))
             if i == 5:
-                quantise("h", FF2, 1)
+                quantise(("h", FF2))
 
         acc_b = {}
         acc_2 = {}
         gate = {}
         dif = {}
         prod = {}
-        for i in range(n_u + 3):
+        for i in range(n_u + 4):
             if i < n_u:
                 acc_b[i] = head_group(TB, units[i])
                 acc_2[i] = head_group(FF2, units[i])
-            if 3 <= i:
-                k = i - 3
+            if 4 <= i:
+                k = i - 4
                 ot = psum.tile([P, 4, P], F32, name="ot", tag="bank")
                 for tt in range(4):
                     cols = slice(128 * tt, 128 * tt + 128)
@@ -376,11 +350,14 @@ def tile_cfccell_pa_kernel(
                 k = i - 1
                 dif[k] = work.tile([P, WIDE], F32, name="dif", tag="dif")
                 nc.vector.tensor_sub(out=dif[k][:], in0=ff2[:], in1=ff1[k][:])
-            if 3 <= i:
-                k = i - 3
+            if 4 <= i:
+                k = i - 4
                 hq, n = units[k]
                 ost = stp.tile([P, 4, P], F32, name="ost", tag="ost")
-                nc.scalar.copy(out=ost[:], in_=ot[:])
+                if k == n_u - 2:
+                    nc.vector.tensor_copy(out=ost[:], in_=ot[:])
+                else:
+                    nc.scalar.copy(out=ost[:], in_=ot[:])
                 nc.sync.dma_start(
                     out=outf[WIDE * n : WIDE * n + WIDE, 128 * hq : 128 * hq + 128].rearrange(
                         "(t p) h -> p t h", p=P

@@ -39,7 +39,7 @@ def tile_cfccell_pa_kernel(
         grp = ctx.enter_context(tc.tile_pool(name="grp", bufs=5))
         thp = ctx.enter_context(tc.tile_pool(name="thp", bufs=2))
         work = ctx.enter_context(tc.tile_pool(name="work", bufs=3))
-        stp = ctx.enter_context(tc.tile_pool(name="stp", bufs=4))
+        stp = ctx.enter_context(tc.tile_pool(name="stp", bufs=6))
         psum = ctx.enter_context(tc.psum_pool(name="psum", bufs=8))
 
         warm = keep.tile([P, 1], F32, name="warm")
@@ -50,6 +50,8 @@ def tile_cfccell_pa_kernel(
         nc.vector.memset(ts_rows[:], 0.0)
         ones = keep.tile([P, P], BF16, name="ones")
         nc.vector.memset(ones[:], 1.0)
+        b1_rows = keep.tile([P, P], BF16, name="b1_rows")
+        nc.vector.memset(b1_rows[:], 0.0)
         bias_rows = keep.tile([P, P], BF16, name="bias_rows")
         nc.vector.memset(bias_rows[:], 0.0)
         ident_f = keep.tile([P, P], F32, name="ident_f")
@@ -96,18 +98,12 @@ def tile_cfccell_pa_kernel(
         load_h1(0, 0)
         load_w1(1, 0)
         load_h1(0, 1)
-        nc.sync.dma_start(out=bias_rows[0:8, :], in_=b1.rearrange("(r c) -> r c", c=P))
-        for h in range(4):
-            nc.sync.dma_start(
-                out=bias_rows[8 + 4 * h : 12 + 4 * h, :],
-                in_=head_b[h].rearrange("(r c) -> r c", c=P),
-            )
-        nc.sync.dma_start(out=ts_rows[0:1, :], in_=ts_row.rearrange("(o t) -> o t", o=1))
+        nc.sync.dma_start(out=b1_rows[0:8, :], in_=b1.rearrange("(r c) -> r c", c=P))
         load_w1(0, 1)
         load_w1(1, 1)
+        load_head(FF1)
         load_h1(1, 0)
         load_h1(1, 1)
-        load_head(FF1)
         load_head(TA)
 
         grouped = {}
@@ -133,15 +129,19 @@ def tile_cfccell_pa_kernel(
             regroup(True, key, g, 0, WIDE // 2)
             regroup(False, key, g, WIDE // 2, WIDE)
 
-        def quantise(key):
-            codes = keep.tile([P, PASSES * WIDE], U32, name="c_%s%d" % key, align_bytes=64)
-            scales = keep.tile([P, PASSES * WIDE], U8, name="s_%s%d" % key, align_bytes=64)
+        def quantise(key, first=0, last=PASSES - 1):
+            if key not in quant:
+                quant[key] = (
+                    keep.tile([P, PASSES * WIDE], U32, name="c_%s%d" % key, align_bytes=64),
+                    keep.tile([P, PASSES * WIDE], U8, name="s_%s%d" % key, align_bytes=64),
+                )
+            codes, scales = quant[key]
+            cols = slice(WIDE * first, WIDE * (last + 1))
             nc.vector.quantize_mx(
-                out=codes[:].bitcast(FP8X4),
-                scales=scales[:],
-                in_=grouped[key][:].rearrange("p g c -> p (g c)"),
+                out=codes[:, cols].bitcast(FP8X4),
+                scales=scales[:, cols],
+                in_=grouped[key][:, first : last + 1, :].rearrange("p g c -> p (g c)"),
             )
-            quant[key] = (codes, scales)
 
         def mx_group(stat, tile_no, mov):
             acc = psum.tile([P, WIDE], F32, name="acc", tag="bank")
@@ -211,44 +211,43 @@ def tile_cfccell_pa_kernel(
             return mx_group(("h", h), hq, ("x", n))
 
         def bias_col(h, hq):
-            c = 8 + 4 * h + hq
+            c = 4 * h + hq
             return bias_t[:, c : c + 1]
 
         h1_transposes(0, 0)
         split(("w", 0), 0)
+        quantise(("w", 0), 0, 0)
         regroup(False, ("w", 0), 1, 0, WIDE)
         h1_out(0, 0)
         h1_transposes(0, 1)
-        quantise(("w", 0))
+        quantise(("w", 0), 1, 1)
         h1_out(0, 1)
-        quantise(("a", 0))
+        quantise(("a", 0), 0, 0)
+        quantise(("a", 0), 1, 1)
         split(("w", 1), 0)
         split(("w", 1), 1)
         pb = psum.tile([P, P], BF16, name="pb", tag="bank")
-        nc.tensor.transpose(pb[:], bias_rows[:], ident_b[:])
-        bias_t = keep.tile([P, 24], F32, name="bias_t")
-        nc.vector.tensor_copy(out=bias_t[:], in_=pb[:, 0:24])
+        nc.tensor.transpose(pb[:], b1_rows[:], ident_b[:])
         b1s = keep.tile([P, 8], F32, name="b1s")
-        nc.vector.tensor_scalar_mul(out=b1s[:], in0=bias_t[:, 0:8], scalar1=0.666)
+        nc.vector.tensor_scalar_mul(out=b1s[:], in0=pb[:, 0:8], scalar1=0.666)
         stage1_mm(0, 0)
         stage1_tanh(0, 0)
         quantise(("w", 1))
         load_head(TB)
         load_head(FF2)
+        for h in range(4):
+            nc.sync.dma_start(
+                out=bias_rows[4 * h : 4 * h + 4, :], in_=head_b[h].rearrange("(r c) -> r c", c=P)
+            )
+        nc.sync.dma_start(out=ts_rows[0:1, :], in_=ts_row.rearrange("(o t) -> o t", o=1))
         h1_transposes(1, 0)
         h1_transposes(1, 1)
         stage1_mm(0, 1)
         h1_out(1, 0)
         h1_out(1, 1)
         stage1_tanh(0, 1)
-        ts_acc = psum.tile([P, TOK], BF16, name="ts_acc", tag="bank")
-        for n in range(2):
-            nc.tensor.matmul(
-                out=ts_acc[:, WIDE * n : WIDE * n + WIDE], lhsT=ones[:],
-                rhs=ts_rows[:, WIDE * n : WIDE * n + WIDE], start=True, stop=True,
-            )
         regroup(False, ("h", FF1), 0, 0, WIDE)
-        split(("h", FF1), 1)
+        regroup(False, ("h", FF1), 1, 0, WIDE)
         x_regroup(0, 0)
         quantise(("a", 1))
         regroup(False, ("h", TA), 0, 0, WIDE)
@@ -259,12 +258,22 @@ def tile_cfccell_pa_kernel(
         for gv in range(2):
             stage1_mm(1, gv)
             stage1_tanh(1, gv)
+        ts_acc = psum.tile([P, TOK], BF16, name="ts_acc", tag="bank")
+        for n in range(2):
+            nc.tensor.matmul(
+                out=ts_acc[:, WIDE * n : WIDE * n + WIDE], lhsT=ones[:],
+                rhs=ts_rows[:, WIDE * n : WIDE * n + WIDE], start=True, stop=True,
+            )
+        bias_ps = psum.tile([P, P], BF16, name="bias_ps", tag="bank")
+        nc.tensor.transpose(bias_ps[:], bias_rows[:], ident_b[:])
         nc.scalar.copy(out=ts_b[:], in_=ts_acc[:])
+        bias_t = keep.tile([P, 16], F32, name="bias_t")
+        nc.scalar.copy(out=bias_t[:], in_=bias_ps[:, 0:16])
         quantise(("h", TA))
         regroup(False, ("h", TB), 0, 0, WIDE)
         x_regroup(0, 1)
         regroup(True, ("h", TB), 1, 0, WIDE)
-        regroup(False, ("h", FF2), 0, 0, WIDE)
+        split(("h", FF2), 0)
         x_regroup(1, 1)
 
         units = [(hq, n) for n in range(2) for hq in range(4)]
@@ -296,11 +305,18 @@ def tile_cfccell_pa_kernel(
                 )
             if i == 1:
                 quantise(("x", 1))
+            if i == 2:
                 regroup(True, ("h", FF2), 1, 0, WIDE)
-            if i == 4:
+            if i == 3:
                 quantise(("h", TB))
             if i == 5:
                 quantise(("h", FF2))
+
+        whole = [slice(0, WIDE)]
+        halves = [slice(0, WIDE // 2), slice(WIDE // 2, WIDE)]
+
+        def parts(k):
+            return halves if k == n_u - 1 else whole
 
         acc_b = {}
         acc_2 = {}
@@ -313,39 +329,48 @@ def tile_cfccell_pa_kernel(
                 acc_2[i] = head_group(FF2, units[i])
             if 4 <= i:
                 k = i - 4
-                ot = psum.tile([P, 4, P], F32, name="ot", tag="bank")
-                for tt in range(4):
-                    cols = slice(128 * tt, 128 * tt + 128)
-                    nc.tensor.matmul(
-                        out=ot[:, tt, :], lhsT=ff1[k][:, cols], rhs=ident_f[:],
-                        is_transpose=True, start=True, stop=False,
-                    )
-                    nc.tensor.matmul(
-                        out=ot[:, tt, :], lhsT=prod[k][:, cols], rhs=ident_f[:],
-                        is_transpose=True, start=False, stop=True,
-                    )
+                ots = []
+                for part in parts(k):
+                    n_t = (part.stop - part.start) // P
+                    ot = psum.tile([P, n_t, P], F32, name="ot", tag="bank")
+                    for tt in range(n_t):
+                        c0 = part.start + P * tt
+                        nc.tensor.matmul(
+                            out=ot[:, tt, :], lhsT=ff1[k][:, c0 : c0 + P], rhs=ident_f[:],
+                            is_transpose=True, start=True, stop=False,
+                        )
+                        nc.tensor.matmul(
+                            out=ot[:, tt, :], lhsT=prod[k][:, c0 : c0 + P], rhs=ident_f[:],
+                            is_transpose=True, start=False, stop=True,
+                        )
+                    ots.append(ot)
             if 1 <= i <= n_u:
                 k = i - 1
                 hq, n = units[k]
                 z = work.tile([P, WIDE], F32, name="z", tag="z")
-                nc.vector.scalar_tensor_tensor(
-                    out=z[:],
-                    in0=acc_b[k][:],
-                    scalar=bias_col(TB, hq),
-                    in1=v1[k][:],
-                    op0=ALU.add,
-                    op1=ALU.add,
-                )
+                for part in parts(k):
+                    nc.vector.scalar_tensor_tensor(
+                        out=z[:, part],
+                        in0=acc_b[k][:, part],
+                        scalar=bias_col(TB, hq),
+                        in1=v1[k][:, part],
+                        op0=ALU.add,
+                        op1=ALU.add,
+                    )
                 ff2 = work.tile([P, WIDE], F32, name="ff2", tag="ff2")
                 nc.scalar.activation(
                     out=ff2[:], in_=acc_2[k][:], func=ACT.Tanh, bias=bias_col(FF2, hq), scale=1.0
                 )
                 gate[k] = work.tile([P, WIDE], F32, name="gate", tag="gate")
-                nc.scalar.activation(out=gate[k][:], in_=z[:], func=ACT.Sigmoid)
+                for part in parts(k):
+                    nc.scalar.activation(out=gate[k][:, part], in_=z[:, part], func=ACT.Sigmoid)
             if 2 <= i <= n_u + 1:
                 k = i - 2
                 prod[k] = work.tile([P, WIDE], F32, name="e", tag="e")
-                nc.vector.tensor_mul(out=prod[k][:], in0=gate[k][:], in1=dif[k][:])
+                for part in parts(k):
+                    nc.vector.tensor_mul(
+                        out=prod[k][:, part], in0=gate[k][:, part], in1=dif[k][:, part]
+                    )
             if 1 <= i <= n_u:
                 k = i - 1
                 dif[k] = work.tile([P, WIDE], F32, name="dif", tag="dif")
@@ -353,14 +378,17 @@ def tile_cfccell_pa_kernel(
             if 4 <= i:
                 k = i - 4
                 hq, n = units[k]
-                ost = stp.tile([P, 4, P], F32, name="ost", tag="ost")
-                if k == n_u - 2:
-                    nc.vector.tensor_copy(out=ost[:], in_=ot[:])
-                else:
-                    nc.scalar.copy(out=ost[:], in_=ot[:])
-                nc.sync.dma_start(
-                    out=outf[WIDE * n : WIDE * n + WIDE, 128 * hq : 128 * hq + 128].rearrange(
-                        "(t p) h -> p t h", p=P
-                    ),
-                    in_=ost[:],
-                )
+                for p_no, part in enumerate(parts(k)):
+                    n_t = (part.stop - part.start) // P
+                    r0 = WIDE * n + part.start
+                    ost = stp.tile([P, n_t, P], F32, name="ost", tag="ost")
+                    if k == n_u - 2 or p_no == 1:
+                        nc.vector.tensor_copy(out=ost[:], in_=ots[p_no][:])
+                    else:
+                        nc.scalar.copy(out=ost[:], in_=ots[p_no][:])
+                    nc.sync.dma_start(
+                        out=outf[r0 : r0 + P * n_t, 128 * hq : 128 * hq + 128].rearrange(
+                            "(t p) h -> p t h", p=P
+                        ),
+                        in_=ost[:],
+                    )

@@ -105,6 +105,11 @@ def tile_cfccell_pa_kernel(
         load_h1(1, 0)
         load_h1(1, 1)
         load_head(TA)
+        for h in range(4):
+            nc.sync.dma_start(
+                out=bias_rows[4 * h : 4 * h + 4, :], in_=head_b[h].rearrange("(r c) -> r c", c=P)
+            )
+        nc.sync.dma_start(out=ts_rows[0:1, :], in_=ts_row.rearrange("(o t) -> o t", o=1))
 
         grouped = {}
         quant = {}
@@ -235,11 +240,6 @@ def tile_cfccell_pa_kernel(
         quantise(("w", 1))
         load_head(TB)
         load_head(FF2)
-        for h in range(4):
-            nc.sync.dma_start(
-                out=bias_rows[4 * h : 4 * h + 4, :], in_=head_b[h].rearrange("(r c) -> r c", c=P)
-            )
-        nc.sync.dma_start(out=ts_rows[0:1, :], in_=ts_row.rearrange("(o t) -> o t", o=1))
         h1_transposes(1, 0)
         h1_transposes(1, 1)
         stage1_mm(0, 1)

@@ -50,7 +50,7 @@ def tile_cfccell_pa_kernel(
         nc.vector.memset(ts_rows[:], 0.0)
         ones = keep.tile([P, P], BF16, name="ones")
         nc.vector.memset(ones[:], 1.0)
-        b1_rows = keep.tile([P, P], BF16, name="b1_rows")
+        b1_rows = keep.tile([P, WIDE], BF16, name="b1_rows")
         nc.vector.memset(b1_rows[:], 0.0)
         bias_rows = keep.tile([P, P], BF16, name="bias_rows")
         nc.vector.memset(bias_rows[:], 0.0)
@@ -90,7 +90,7 @@ def tile_cfccell_pa_kernel(
                 t_raw = raw.tile([P, 4, H_DIM], BF16, name="hd_raw%d%d" % (h, g), tag="raw")
                 nc.sync.dma_start(
                     out=t_raw[:],
-                    in_=head_w[h][512 * g : 512 * g + 512, :].rearrange("(t p) n -> p t n", p=P),
+                    in_=head_w[h][512 * g : 512 * g + 512, :].rearrange("(p t) n -> p t n", t=4),
                 )
                 hd_raw[(h, g)] = t_raw
 
@@ -98,7 +98,7 @@ def tile_cfccell_pa_kernel(
         load_h1(0, 0)
         load_w1(1, 0)
         load_h1(0, 1)
-        nc.sync.dma_start(out=b1_rows[0:8, :], in_=b1.rearrange("(r c) -> r c", c=P))
+        nc.sync.dma_start(out=b1_rows[0:2, :], in_=b1.rearrange("(r c) -> r c", c=WIDE))
         load_w1(0, 1)
         load_w1(1, 1)
         load_head(FF1)
@@ -122,8 +122,14 @@ def tile_cfccell_pa_kernel(
             return grouped[key]
 
         def regroup(on_scalar, key, g, c0, c1):
-            src = w1_raw[(g, key[1])] if key[0] == "w" else hd_raw[(key[1], g)]
-            dst = group_tile(key)[:, g, 4 * c0 : 4 * c1].rearrange("p (c i t) -> p c t i", i=4, t=4)
+            if key[0] == "w":
+                src = w1_raw[(g, key[1])]
+                dst = group_tile(key)[:, g, :].rearrange("p (i m t) -> p m t i", i=4, t=4)
+                dst = dst[:, c0 // 4 : c1 // 4, :, :]
+            else:
+                src = hd_raw[(key[1], g)]
+                dst = group_tile(key)[:, g, 4 * c0 : 4 * c1]
+                dst = dst.rearrange("p (c i t) -> p c t i", i=4, t=4)
             s_v = src[:, :, c0:c1].rearrange("p t (c i) -> p c t i", i=4)
             if on_scalar:
                 nc.scalar.copy(out=dst, in_=s_v)
@@ -231,10 +237,15 @@ def tile_cfccell_pa_kernel(
         quantise(("a", 0), 1, 1)
         split(("w", 1), 0)
         split(("w", 1), 1)
-        pb = psum.tile([P, P], BF16, name="pb", tag="bank")
-        nc.tensor.transpose(pb[:], b1_rows[:], ident_b[:])
+        pb = psum.tile([P, 4, P], BF16, name="pb", tag="bank")
+        for i in range(4):
+            nc.tensor.transpose(
+                pb[:, i, :], b1_rows[:].rearrange("r (m i) -> r i m", i=4)[:, i, :], ident_b[:]
+            )
         b1s = keep.tile([P, 8], F32, name="b1s")
-        nc.vector.tensor_scalar_mul(out=b1s[:], in0=pb[:, 0:8], scalar1=0.666)
+        nc.vector.tensor_scalar_mul(
+            out=b1s[:].rearrange("p (g i) -> p i g", i=4), in0=pb[:, :, 0:PASSES], scalar1=0.666
+        )
         stage1_mm(0, 0)
         stage1_tanh(0, 0)
         quantise(("w", 1))

@@ -143,8 +143,8 @@ def tile_cfccell_pa_kernel(
         def quantise(key, first=0, last=PASSES - 1):
             if key not in quant:
                 quant[key] = (
-                    keep.tile([P, PASSES * WIDE], U32, name="c_%s%d" % key, align_bytes=64),
-                    keep.tile([P, PASSES * WIDE], U8, name="s_%s%d" % key, align_bytes=64),
+                    keep.tile([P, PASSES * WIDE], U32, name="c_%s%d" % key, align_bytes=256),
+                    keep.tile([P, PASSES * WIDE], U8, name="s_%s%d" % key, align_bytes=256),
                 )
             codes, scales = quant[key]
             cols = slice(WIDE * first, WIDE * (last + 1))
@@ -393,11 +393,13 @@ def tile_cfccell_pa_kernel(
                     n_t = (part.stop - part.start) // P
                     r0 = WIDE * n + part.start
                     ost = stp.tile([P, n_t, P], F32, name="ost", tag="ost")
-                    if k == n_u - 2 or p_no == 1:
+                    on_vector = k == n_u - 2 or (k == n_u - 1 and p_no == 0)
+                    if on_vector:
                         nc.vector.tensor_copy(out=ost[:], in_=ots[p_no][:])
                     else:
                         nc.scalar.copy(out=ost[:], in_=ots[p_no][:])
-                    nc.sync.dma_start(
+                    queue = nc.scalar if p_no == 1 else nc.sync
+                    queue.dma_start(
                         out=outf[r0 : r0 + P * n_t, 128 * hq : 128 * hq + 128].rearrange(
                             "(t p) h -> p t h", p=P
                         ),

@@ -284,7 +284,7 @@ def tile_cfccell_pa_kernel(
         regroup(False, ("h", TB), 0, 0, WIDE)
         x_regroup(0, 1)
         regroup(True, ("h", TB), 1, 0, WIDE)
-        split(("h", FF2), 0)
+        regroup(False, ("h", FF2), 0, 0, WIDE)
         x_regroup(1, 1)
 
         units = [(hq, n) for n in range(2) for hq in range(4)]

@@ -283,8 +283,7 @@ def tile_cfccell_pa_kernel(
         quantise(("h", TA))
         regroup(False, ("h", TB), 0, 0, WIDE)
         x_regroup(0, 1)
-        regroup(True, ("h", TB), 1, 0, WIDE)
-        regroup(False, ("h", FF2), 0, 0, WIDE)
+        regroup(True, ("h", TB), 1, 0, WIDE // 2)
         x_regroup(1, 1)
 
         units = [(hq, n) for n in range(2) for hq in range(4)]
@@ -316,8 +315,13 @@ def tile_cfccell_pa_kernel(
                 )
             if i == 1:
                 quantise(("x", 1))
+                regroup(False, ("h", FF2), 0, 0, WIDE)
+            if i == 1:
+                regroup(True, ("h", TB), 1, WIDE // 2, WIDE)
             if i == 2:
-                regroup(True, ("h", FF2), 1, 0, WIDE)
+                regroup(True, ("h", FF2), 1, 0, WIDE // 2)
+            if i == 4:
+                regroup(True, ("h", FF2), 1, WIDE // 2, WIDE)
             if i == 3:
                 quantise(("h", TB))
             if i == 5:

@@ -38,7 +38,7 @@ def tile_cfccell_pa_kernel(
         raw = ctx.enter_context(tc.tile_pool(name="raw", bufs=12))
         grp = ctx.enter_context(tc.tile_pool(name="grp", bufs=5))
         thp = ctx.enter_context(tc.tile_pool(name="thp", bufs=2))
-        work = ctx.enter_context(tc.tile_pool(name="work", bufs=3))
+        work = ctx.enter_context(tc.tile_pool(name="work", bufs=4))
         stp = ctx.enter_context(tc.tile_pool(name="stp", bufs=6))
         psum = ctx.enter_context(tc.psum_pool(name="psum", bufs=8))
 
@@ -185,10 +185,10 @@ def tile_cfccell_pa_kernel(
                         )
                 h1_banks[(n, g, pair)] = bank
 
-        def h1_out(n, pair):
-            for g in range(PASSES):
+        def h1_out(n, pair, gs=(0, 1), eng=nc.scalar.copy):
+            for g in gs:
                 hgw = group_tile(("a", n))[:, g, :].bitcast(F32).rearrange("p (r u) -> p r u", u=2)
-                nc.scalar.copy(
+                eng(
                     out=hgw[:, 256 * pair : 256 * pair + 256, :],
                     in_=h1_banks[(n, g, pair)][:].rearrange("p u r -> p r u"),
                 )
@@ -233,10 +233,6 @@ def tile_cfccell_pa_kernel(
         h1_transposes(0, 1)
         quantise(("w", 0), 1, 1)
         h1_out(0, 1)
-        quantise(("a", 0), 0, 0)
-        quantise(("a", 0), 1, 1)
-        split(("w", 1), 0)
-        split(("w", 1), 1)
         pb = psum.tile([P, 4, P], BF16, name="pb", tag="bank")
         for i in range(4):
             nc.tensor.transpose(
@@ -246,6 +242,10 @@ def tile_cfccell_pa_kernel(
         nc.vector.tensor_scalar_mul(
             out=b1s[:].rearrange("p (g i) -> p i g", i=4), in0=pb[:, :, 0:PASSES], scalar1=0.666
         )
+        quantise(("a", 0), 0, 0)
+        quantise(("a", 0), 1, 1)
+        split(("w", 1), 0)
+        split(("w", 1), 1)
         stage1_mm(0, 0)
         stage1_tanh(0, 0)
         quantise(("w", 1))
@@ -260,10 +260,10 @@ def tile_cfccell_pa_kernel(
         regroup(False, ("h", FF1), 0, 0, WIDE)
         regroup(False, ("h", FF1), 1, 0, WIDE)
         x_regroup(0, 0)
-        quantise(("a", 1))
         regroup(False, ("h", TA), 0, 0, WIDE)
-        x_regroup(1, 0)
+        quantise(("a", 1))
         quantise(("h", FF1))
+        x_regroup(1, 0)
         quantise(("x", 0))
         regroup(True, ("h", TA), 1, 0, WIDE)
         for gv in range(2):
@@ -333,6 +333,7 @@ def tile_cfccell_pa_kernel(
         def parts(k):
             return halves if k == n_u - 1 else whole
 
+        ots = {}
         acc_b = {}
         acc_2 = {}
         gate = {}
@@ -342,9 +343,9 @@ def tile_cfccell_pa_kernel(
             if i < n_u:
                 acc_b[i] = head_group(TB, units[i])
                 acc_2[i] = head_group(FF2, units[i])
-            if 4 <= i:
-                k = i - 4
-                ots = []
+            if 3 <= i < n_u + 3:
+                k = i - 3
+                ots[k] = []
                 for part in parts(k):
                     n_t = (part.stop - part.start) // P
                     ot = psum.tile([P, n_t, P], F32, name="ot", tag="bank")
@@ -358,7 +359,7 @@ def tile_cfccell_pa_kernel(
                             out=ot[:, tt, :], lhsT=prod[k][:, c0 : c0 + P], rhs=ident_f[:],
                             is_transpose=True, start=False, stop=True,
                         )
-                    ots.append(ot)
+                    ots[k].append(ot)
             if 1 <= i <= n_u:
                 k = i - 1
                 hq, n = units[k]
@@ -376,20 +377,6 @@ def tile_cfccell_pa_kernel(
                 nc.scalar.activation(
                     out=ff2[:], in_=acc_2[k][:], func=ACT.Tanh, bias=bias_col(FF2, hq), scale=1.0
                 )
-                gate[k] = work.tile([P, WIDE], F32, name="gate", tag="gate")
-                for part in parts(k):
-                    nc.scalar.activation(out=gate[k][:, part], in_=z[:, part], func=ACT.Sigmoid)
-            if 2 <= i <= n_u + 1:
-                k = i - 2
-                prod[k] = work.tile([P, WIDE], F32, name="e", tag="e")
-                for part in parts(k):
-                    nc.vector.tensor_mul(
-                        out=prod[k][:, part], in0=gate[k][:, part], in1=dif[k][:, part]
-                    )
-            if 1 <= i <= n_u:
-                k = i - 1
-                dif[k] = work.tile([P, WIDE], F32, name="dif", tag="dif")
-                nc.vector.tensor_sub(out=dif[k][:], in0=ff2[:], in1=ff1[k][:])
             if 4 <= i:
                 k = i - 4
                 hq, n = units[k]
@@ -397,11 +384,7 @@ def tile_cfccell_pa_kernel(
                     n_t = (part.stop - part.start) // P
                     r0 = WIDE * n + part.start
                     ost = stp.tile([P, n_t, P], F32, name="ost", tag="ost")
-                    on_vector = k == n_u - 2 or (k == n_u - 1 and p_no == 0)
-                    if on_vector:
-                        nc.vector.tensor_copy(out=ost[:], in_=ots[p_no][:])
-                    else:
-                        nc.scalar.copy(out=ost[:], in_=ots[p_no][:])
+                    nc.scalar.copy(out=ost[:], in_=ots[k][p_no][:])
                     queue = nc.scalar if p_no == 1 else nc.sync
                     queue.dma_start(
                         out=outf[r0 : r0 + P * n_t, 128 * hq : 128 * hq + 128].rearrange(
@@ -409,3 +392,19 @@ def tile_cfccell_pa_kernel(
                         ),
                         in_=ost[:],
                     )
+            if 1 <= i <= n_u:
+                k = i - 1
+                gate[k] = z
+                for part in parts(k):
+                    nc.scalar.activation(out=gate[k][:, part], in_=z[:, part], func=ACT.Sigmoid)
+            if 2 <= i <= n_u + 1:
+                k = i - 2
+                prod[k] = v1[k]
+                for part in parts(k):
+                    nc.vector.tensor_mul(
+                        out=prod[k][:, part], in0=gate[k][:, part], in1=dif[k][:, part]
+                    )
+            if 1 <= i <= n_u:
+                k = i - 1
+                dif[k] = ff2
+                nc.vector.tensor_sub(out=dif[k][:], in0=ff2[:], in1=ff1[k][:])

@@ -46,10 +46,6 @@ def tile_cfccell_pa_kernel(
         nc.vector.memset(warm[:], 0.0)
         warm_out = keep.tile([P, 1], F32, name="warm_out")
         nc.scalar.activation(out=warm_out[:], in_=warm[:], func=ACT.Sigmoid)
-        ts_rows = keep.tile([P, TOK], BF16, name="ts_rows")
-        nc.vector.memset(ts_rows[:], 0.0)
-        ones = keep.tile([P, P], BF16, name="ones")
-        nc.vector.memset(ones[:], 1.0)
         b1_rows = keep.tile([P, WIDE], BF16, name="b1_rows")
         nc.vector.memset(b1_rows[:], 0.0)
         bias_rows = keep.tile([P, P], BF16, name="bias_rows")
@@ -109,7 +105,6 @@ def tile_cfccell_pa_kernel(
             nc.sync.dma_start(
                 out=bias_rows[4 * h : 4 * h + 4, :], in_=head_b[h].rearrange("(r c) -> r c", c=P)
             )
-        nc.sync.dma_start(out=ts_rows[0:1, :], in_=ts_row.rearrange("(o t) -> o t", o=1))
 
         grouped = {}
         quant = {}
@@ -233,6 +228,10 @@ def tile_cfccell_pa_kernel(
         h1_transposes(0, 1)
         quantise(("w", 0), 1, 1)
         h1_out(0, 1)
+        quantise(("a", 0), 0, 0)
+        quantise(("a", 0), 1, 1)
+        split(("w", 1), 0)
+        split(("w", 1), 1)
         pb = psum.tile([P, 4, P], BF16, name="pb", tag="bank")
         for i in range(4):
             nc.tensor.transpose(
@@ -242,15 +241,12 @@ def tile_cfccell_pa_kernel(
         nc.vector.tensor_scalar_mul(
             out=b1s[:].rearrange("p (g i) -> p i g", i=4), in0=pb[:, :, 0:PASSES], scalar1=0.666
         )
-        quantise(("a", 0), 0, 0)
-        quantise(("a", 0), 1, 1)
-        split(("w", 1), 0)
-        split(("w", 1), 1)
         stage1_mm(0, 0)
         stage1_tanh(0, 0)
         quantise(("w", 1))
         load_head(TB)
         load_head(FF2)
+        nc.sync.dma_start(out=ts_b[:], in_=ts_row.partition_broadcast(P))
         h1_transposes(1, 0)
         h1_transposes(1, 1)
         stage1_mm(0, 1)
@@ -260,24 +256,17 @@ def tile_cfccell_pa_kernel(
         regroup(False, ("h", FF1), 0, 0, WIDE)
         regroup(False, ("h", FF1), 1, 0, WIDE)
         x_regroup(0, 0)
-        regroup(False, ("h", TA), 0, 0, WIDE)
         quantise(("a", 1))
-        quantise(("h", FF1))
+        regroup(False, ("h", TA), 0, 0, WIDE)
         x_regroup(1, 0)
+        quantise(("h", FF1))
         quantise(("x", 0))
         regroup(True, ("h", TA), 1, 0, WIDE)
         for gv in range(2):
             stage1_mm(1, gv)
             stage1_tanh(1, gv)
-        ts_acc = psum.tile([P, TOK], BF16, name="ts_acc", tag="bank")
-        for n in range(2):
-            nc.tensor.matmul(
-                out=ts_acc[:, WIDE * n : WIDE * n + WIDE], lhsT=ones[:],
-                rhs=ts_rows[:, WIDE * n : WIDE * n + WIDE], start=True, stop=True,
-            )
         bias_ps = psum.tile([P, P], BF16, name="bias_ps", tag="bank")
         nc.tensor.transpose(bias_ps[:], bias_rows[:], ident_b[:])
-        nc.scalar.copy(out=ts_b[:], in_=ts_acc[:])
         bias_t = keep.tile([P, 16], F32, name="bias_t")
         nc.scalar.copy(out=bias_t[:], in_=bias_ps[:, 0:16])
         quantise(("h", TA))
@@ -315,7 +304,8 @@ def tile_cfccell_pa_kernel(
                 )
             if i == 1:
                 quantise(("x", 1))
-                regroup(False, ("h", FF2), 0, 0, WIDE)
+                regroup(True, ("h", FF2), 0, 0, 128)
+                regroup(False, ("h", FF2), 0, 128, WIDE)
             if i == 1:
                 regroup(True, ("h", TB), 1, WIDE // 2, WIDE)
             if i == 2:
@@ -384,7 +374,11 @@ def tile_cfccell_pa_kernel(
                     n_t = (part.stop - part.start) // P
                     r0 = WIDE * n + part.start
                     ost = stp.tile([P, n_t, P], F32, name="ost", tag="ost")
-                    nc.scalar.copy(out=ost[:], in_=ots[k][p_no][:])
+                    on_vector = k == n_u - 1 and p_no == 0
+                    if on_vector:
+                        nc.vector.tensor_copy(out=ost[:], in_=ots[k][p_no][:])
+                    else:
+                        nc.scalar.copy(out=ost[:], in_=ots[k][p_no][:])
                     queue = nc.scalar if p_no == 1 else nc.sync
                     queue.dma_start(
                         out=outf[r0 : r0 + P * n_t, 128 * hq : 128 * hq + 128].rearrange(

from contextlib import ExitStack

import concourse.mybir as mybir
from concourse.masks import make_identity

F32 = mybir.dt.float32
BF16 = mybir.dt.bfloat16
U32 = mybir.dt.uint32
U8 = mybir.dt.uint8
FP8X4 = mybir.dt.float8_e4m3fn_x4
ACT = mybir.ActivationFunctionType
ALU = mybir.AluOpType

P = 128
TOK = 1024
U_DIM = 1024
V_DIM = 1024
H_DIM = 512
WIDE = 512
PASSES = 2
FLOPS = 2 * TOK * U_DIM * V_DIM + 4 * 2 * TOK * V_DIM * H_DIM

FF1, FF2, TA, TB = 0, 1, 2, 3


def tile_cfccell_pa_kernel(
    tc, h1, ts, W1, b1, W_ff1, b_ff1, W_ff2, b_ff2, W_ta, b_ta, W_tb, b_tb, out
):
    nc = tc.nc
    h1f = h1.flatten_outer_dims()
    outf = out.flatten_outer_dims()
    ts_row = ts.rearrange("b t -> (b t)")
    head_w = [W_ff1, W_ff2, W_ta, W_tb]
    head_b = [b_ff1, b_ff2, b_ta, b_tb]

    with ExitStack() as ctx:
        keep = ctx.enter_context(tc.tile_pool(name="keep", bufs=1))
        raw = ctx.enter_context(tc.tile_pool(name="raw", bufs=12))
        grp = ctx.enter_context(tc.tile_pool(name="grp", bufs=5))
        thp = ctx.enter_context(tc.tile_pool(name="thp", bufs=2))
        work = ctx.enter_context(tc.tile_pool(name="work", bufs=4))
        stp = ctx.enter_context(tc.tile_pool(name="stp", bufs=6))
        psum = ctx.enter_context(tc.psum_pool(name="psum", bufs=8))

        warm = keep.tile([P, 1], F32, name="warm")
        nc.vector.memset(warm[:], 0.0)
        warm_out = keep.tile([P, 1], F32, name="warm_out")
        nc.scalar.activation(out=warm_out[:], in_=warm[:], func=ACT.Sigmoid)
        b1_rows = keep.tile([P, WIDE], BF16, name="b1_rows")
        nc.vector.memset(b1_rows[:], 0.0)
        bias_rows = keep.tile([P, P], BF16, name="bias_rows")
        nc.vector.memset(bias_rows[:], 0.0)
        ident_f = keep.tile([P, P], F32, name="ident_f")
        make_identity(nc, ident_f[:])
        ident_b = keep.tile([P, P], BF16, name="ident_b")
        make_identity(nc, ident_b[:])
        ts_b = keep.tile([P, TOK], BF16, name="ts_b")
        ctx.enter_context(tc.manual_schedule())

        w1_raw = {}
        h1_raw = {}
        hd_raw = {}

        def load_w1(g, half):
            t_raw = raw.tile([P, 4, WIDE], BF16, name="w1_raw%d%d" % (g, half), tag="raw")
            for u in range(2):
                r0 = 512 * g + 256 * u
                nc.sync.dma_start(
                    out=t_raw[:, 2 * u : 2 * u + 2, :],
                    in_=W1[r0 : r0 + 256, WIDE * half : WIDE * half + WIDE].rearrange(
                        "(q e) c -> q e c", e=2
                    ),
                )
            w1_raw[(g, half)] = t_raw

        def load_h1(n, pair):
            t_raw = raw.tile([P, 2, U_DIM], BF16, name="h1_raw%d%d" % (n, pair), tag="raw")
            r0 = WIDE * n + 256 * pair
            nc.sync.dma_start(
                out=t_raw[:], in_=h1f[r0 : r0 + 256, :].rearrange("(t p) u -> p t u", p=P)
            )
            h1_raw[(n, pair)] = t_raw

        def load_head(h):
            for g in range(PASSES):
                t_raw = raw.tile([P, 4, H_DIM], BF16, name="hd_raw%d%d" % (h, g), tag="raw")
                nc.sync.dma_start(
                    out=t_raw[:],
                    in_=head_w[h][512 * g : 512 * g + 512, :].rearrange("(p t) n -> p t n", t=4),
                )
                hd_raw[(h, g)] = t_raw

        load_w1(0, 0)
        load_h1(0, 0)
        load_w1(1, 0)
        load_h1(0, 1)
        nc.sync.dma_start(out=b1_rows[0:2, :], in_=b1.rearrange("(r c) -> r c", c=WIDE))
        load_w1(0, 1)
        load_w1(1, 1)
        load_head(FF1)
        load_h1(1, 0)
        load_h1(1, 1)
        load_head(TA)
        for h in range(4):
            nc.sync.dma_start(
                out=bias_rows[4 * h : 4 * h + 4, :], in_=head_b[h].rearrange("(r c) -> r c", c=P)
            )

        grouped = {}
        quant = {}

        def group_tile(key):
            if key not in grouped:
                grouped[key] = grp.tile(
                    [P, PASSES, 4 * WIDE], BF16, name="g_%s%d" % key, tag="grp", align_bytes=64
                )
            return grouped[key]

        def regroup(on_scalar, key, g, c0, c1):
            if key[0] == "w":
                src = w1_raw[(g, key[1])]
                dst = group_tile(key)[:, g, :].rearrange("p (i m t) -> p m t i", i=4, t=4)
                dst = dst[:, c0 // 4 : c1 // 4, :, :]
            else:
                src = hd_raw[(key[1], g)]
                dst = group_tile(key)[:, g, 4 * c0 : 4 * c1]
                dst = dst.rearrange("p (c i t) -> p c t i", i=4, t=4)
            s_v = src[:, :, c0:c1].rearrange("p t (c i) -> p c t i", i=4)
            if on_scalar:
                nc.scalar.copy(out=dst, in_=s_v)
            else:
                nc.vector.tensor_copy(out=dst, in_=s_v)

        def split(key, g):
            regroup(True, key, g, 0, WIDE // 2)
            regroup(False, key, g, WIDE // 2, WIDE)

        def quantise(key, first=0, last=PASSES - 1):
            if key not in quant:
                quant[key] = (
                    keep.tile([P, PASSES * WIDE], U32, name="c_%s%d" % key, align_bytes=256),
                    keep.tile([P, PASSES * WIDE], U8, name="s_%s%d" % key, align_bytes=256),
                )
            codes, scales = quant[key]
            cols = slice(WIDE * first, WIDE * (last + 1))
            nc.vector.quantize_mx(
                out=codes[:, cols].bitcast(FP8X4),
                scales=scales[:, cols],
                in_=grouped[key][:, first : last + 1, :].rearrange("p g c -> p (g c)"),
            )

        def mx_group(stat, tile_no, mov):
            acc = psum.tile([P, WIDE], F32, name="acc", tag="bank")
            for g in range(PASSES):
                s0 = WIDE * g + P * tile_no
                m_cols = slice(WIDE * g, WIDE * g + WIDE)
                nc.tensor.matmul_mx(
                    out=acc[:],
                    lhsT=quant[stat][0][:, s0 : s0 + P].bitcast(FP8X4),
                    lhsT_scale=quant[stat][1][:, s0 : s0 + P],
                    rhs=quant[mov][0][:, m_cols].bitcast(FP8X4),
                    rhs_scale=quant[mov][1][:, m_cols],
                    start=(g == 0),
                    stop=(g == PASSES - 1),
                )
            return acc

        h1_banks = {}

        def h1_transposes(n, pair):
            for g in range(PASSES):
                bank = psum.tile([P, 2, 256], F32, name="h1t", tag="bank")
                for u in range(2):
                    for j in range(2):
                        c0 = 256 * g + 128 * u
                        nc.tensor.transpose(
                            bank[:, u, 128 * j : 128 * j + 128],
                            h1_raw[(n, pair)][:, j, :].bitcast(F32)[:, c0 : c0 + 128],
                            ident_f[:],
                        )
                h1_banks[(n, g, pair)] = bank

        def h1_out(n, pair, gs=(0, 1), eng=nc.scalar.copy):
            for g in gs:
                hgw = group_tile(("a", n))[:, g, :].bitcast(F32).rearrange("p (r u) -> p r u", u=2)
                eng(
                    out=hgw[:, 256 * pair : 256 * pair + 256, :],
                    in_=h1_banks[(n, g, pair)][:].rearrange("p u r -> p r u"),
                )

        acc_x = {}
        tanh_x = {}

        def stage1_mm(n, gv):
            for t in range(4):
                acc_x[(n, gv, t)] = mx_group(("w", gv), t, ("a", n))

        def stage1_tanh(n, gv):
            th = thp.tile([P, 4, WIDE], F32, name="th", tag="th")
            for t in range(4):
                m = 4 * gv + t
                nc.scalar.activation(
                    out=th[:, t, :], in_=acc_x[(n, gv, t)][:], func=ACT.Tanh,
                    bias=b1s[:, m : m + 1], scale=0.666,
                )
            tanh_x[(gv, n)] = th

        def x_regroup(gv, n):
            nc.vector.tensor_scalar_mul(
                out=group_tile(("x", n))[:, gv, :].rearrange("p (r i t) -> p r t i", i=4, t=4),
                in0=tanh_x[(gv, n)][:].rearrange("p t (r i) -> p r t i", i=4),
                scalar1=1.7159,
            )

        def head_group(h, unit):
            hq, n = unit
            return mx_group(("h", h), hq, ("x", n))

        def bias_col(h, hq):
            c = 4 * h + hq
            return bias_t[:, c : c + 1]

        h1_transposes(0, 0)
        split(("w", 0), 0)
        quantise(("w", 0), 0, 0)
        regroup(False, ("w", 0), 1, 0, WIDE)
        h1_out(0, 0)
        h1_transposes(0, 1)
        quantise(("w", 0), 1, 1)
        h1_out(0, 1)
        quantise(("a", 0), 0, 0)
        quantise(("a", 0), 1, 1)
        split(("w", 1), 0)
        split(("w", 1), 1)
        pb = psum.tile([P, 4, P], BF16, name="pb", tag="bank")
        for i in range(4):
            nc.tensor.transpose(
                pb[:, i, :], b1_rows[:].rearrange("r (m i) -> r i m", i=4)[:, i, :], ident_b[:]
            )
        b1s = keep.tile([P, 8], F32, name="b1s")
        nc.vector.tensor_scalar_mul(
            out=b1s[:].rearrange("p (g i) -> p i g", i=4), in0=pb[:, :, 0:PASSES], scalar1=0.666
        )
        stage1_mm(0, 0)
        stage1_tanh(0, 0)
        quantise(("w", 1))
        load_head(TB)
        load_head(FF2)
        nc.sync.dma_start(out=ts_b[:], in_=ts_row.partition_broadcast(P))
        h1_transposes(1, 0)
        h1_transposes(1, 1)
        stage1_mm(0, 1)
        h1_out(1, 0)
        h1_out(1, 1)
        stage1_tanh(0, 1)
        regroup(False, ("h", FF1), 0, 0, WIDE)
        regroup(False, ("h", FF1), 1, 0, WIDE)
        x_regroup(0, 0)
        quantise(("a", 1))
        regroup(False, ("h", TA), 0, 0, WIDE)
        x_regroup(1, 0)
        quantise(("h", FF1))
        quantise(("x", 0))
        regroup(True, ("h", TA), 1, 0, WIDE)
        for gv in range(2):
            stage1_mm(1, gv)
            stage1_tanh(1, gv)
        bias_ps = psum.tile([P, P], BF16, name="bias_ps", tag="bank")
        nc.tensor.transpose(bias_ps[:], bias_rows[:], ident_b[:])
        bias_t = keep.tile([P, 16], F32, name="bias_t")
        nc.scalar.copy(out=bias_t[:], in_=bias_ps[:, 0:16])
        quantise(("h", TA))
        regroup(False, ("h", TB), 0, 0, WIDE)
        x_regroup(0, 1)
        regroup(True, ("h", TB), 1, 0, WIDE // 2)
        x_regroup(1, 1)

        units = [(hq, n) for n in range(2) for hq in range(4)]
        n_u = len(units)

        ff1 = {}
        v1 = {}
        acc_f = {}
        acc_a = {}
        for i in range(n_u + 1):
            if i < n_u:
                acc_f[i] = head_group(FF1, units[i])
                acc_a[i] = head_group(TA, units[i])
            if i >= 1:
                k = i - 1
                hq, n = units[k]
                ff1[k] = keep.tile([P, WIDE], F32, name="ff1_%d" % k)
                nc.scalar.activation(
                    out=ff1[k][:], in_=acc_f[k][:], func=ACT.Tanh, bias=bias_col(FF1, hq), scale=1.0
                )
                v1[k] = keep.tile([P, WIDE], F32, name="v1_%d" % k)
                nc.vector.scalar_tensor_tensor(
                    out=v1[k][:],
                    in0=acc_a[k][:],
                    scalar=bias_col(TA, hq),
                    in1=ts_b[:, WIDE * n : WIDE * n + WIDE],
                    op0=ALU.add,
                    op1=ALU.mult,
                )
            if i == 1:
                quantise(("x", 1))
                regroup(True, ("h", FF2), 0, 0, 128)
                regroup(False, ("h", FF2), 0, 128, WIDE)
            if i == 1:
                regroup(True, ("h", TB), 1, WIDE // 2, WIDE)
            if i == 2:
                regroup(True, ("h", FF2), 1, 0, WIDE // 2)
            if i == 4:
                regroup(True, ("h", FF2), 1, WIDE // 2, WIDE)
            if i == 3:
                quantise(("h", TB))
            if i == 5:
                quantise(("h", FF2))

        whole = [slice(0, WIDE)]
        halves = [slice(0, WIDE // 2), slice(WIDE // 2, WIDE)]

        def parts(k):
            return halves if k == n_u - 1 else whole

        ots = {}
        acc_b = {}
        acc_2 = {}
        gate = {}
        dif = {}
        prod = {}
        for i in range(n_u + 4):
            if i < n_u:
                acc_b[i] = head_group(TB, units[i])
                acc_2[i] = head_group(FF2, units[i])
            if 3 <= i < n_u + 3:
                k = i - 3
                ots[k] = []
                for part in parts(k):
                    n_t = (part.stop - part.start) // P
                    ot = psum.tile([P, n_t, P], F32, name="ot", tag="bank")
                    for tt in range(n_t):
                        c0 = part.start + P * tt
                        nc.tensor.matmul(
                            out=ot[:, tt, :], lhsT=ff1[k][:, c0 : c0 + P], rhs=ident_f[:],
                            is_transpose=True, start=True, stop=False,
                        )
                        nc.tensor.matmul(
                            out=ot[:, tt, :], lhsT=prod[k][:, c0 : c0 + P], rhs=ident_f[:],
                            is_transpose=True, start=False, stop=True,
                        )
                    ots[k].append(ot)
            if 1 <= i <= n_u:
                k = i - 1
                hq, n = units[k]
                z = work.tile([P, WIDE], F32, name="z", tag="z")
                for part in parts(k):
                    nc.vector.scalar_tensor_tensor(
                        out=z[:, part],
                        in0=acc_b[k][:, part],
                        scalar=bias_col(TB, hq),
                        in1=v1[k][:, part],
                        op0=ALU.add,
                        op1=ALU.add,
                    )
                ff2 = work.tile([P, WIDE], F32, name="ff2", tag="ff2")
                nc.scalar.activation(
                    out=ff2[:], in_=acc_2[k][:], func=ACT.Tanh, bias=bias_col(FF2, hq), scale=1.0
                )
            if 4 <= i:
                k = i - 4
                hq, n = units[k]
                for p_no, part in enumerate(parts(k)):
                    n_t = (part.stop - part.start) // P
                    r0 = WIDE * n + part.start
                    ost = stp.tile([P, n_t, P], F32, name="ost", tag="ost")
                    on_vector = k == n_u - 1 and p_no == 0
                    if on_vector:
                        nc.vector.tensor_copy(out=ost[:], in_=ots[k][p_no][:])
                    else:
                        nc.scalar.copy(out=ost[:], in_=ots[k][p_no][:])
                    queue = nc.scalar if p_no == 1 else nc.sync
                    queue.dma_start(
                        out=outf[r0 : r0 + P * n_t, 128 * hq : 128 * hq + 128].rearrange(
                            "(t p) h -> p t h", p=P
                        ),
                        in_=ost[:],
                    )
            if 1 <= i <= n_u:
                k = i - 1
                gate[k] = z
                for part in parts(k):
                    nc.scalar.activation(out=gate[k][:, part], in_=z[:, part], func=ACT.Sigmoid)
            if 2 <= i <= n_u + 1:
                k = i - 2
                prod[k] = v1[k]
                for part in parts(k):
                    nc.vector.tensor_mul(
                        out=prod[k][:, part], in0=gate[k][:, part], in1=dif[k][:, part]
                    )
            if 1 <= i <= n_u:
                k = i - 1
                dif[k] = ff2
                nc.vector.tensor_sub(out=dif[k][:], in0=ff2[:], in1=ff1[k][:])
